import numpy as np
import ml_dtypes


def mxq(x, axis, fmt="e4m3"):
    dtype, down = {"e4m3": (ml_dtypes.float8_e4m3fn, 7), "e5m2": (ml_dtypes.float8_e5m2, 14)}[fmt]
    v = np.moveaxis(np.asarray(x, np.float32).astype(ml_dtypes.bfloat16).astype(np.float64), axis, -1)
    blocks = v.reshape(v.shape[:-1] + (-1, 32))
    amax = np.abs(blocks).max(-1, keepdims=True)
    byte = np.maximum(np.where(amax > 0, np.frexp(amax)[1] - 1 + 127, 0) - down, 1)
    scale = np.exp2(byte - 127.0)
    codes = (blocks / scale).astype(np.float32).astype(dtype).astype(np.float64)
    return np.moveaxis((codes * scale).reshape(v.shape), -1, axis)


WIDE = False


def mx_kscale(k):
    if not WIDE:
        return np.ones(k)
    levels = np.array([10, -10, 5, -5, 0])
    a = np.random.permutation(np.resize(levels, k // 512 * 4)).reshape(k // 512, 4)
    idx = np.arange(k)
    return np.exp2(a[idx // 512, idx % 128 // 32])


BF16 = ml_dtypes.bfloat16


def bf(x):
    return np.asarray(x, np.float32).astype(BF16)


def f64(x):
    return np.asarray(x).astype(np.float64)


E2M1 = np.array([0.0, 0.5, 1.0, 1.5, 2.0, 3.0, 4.0, 6.0, -0.0, -0.5, -1.0, -1.5, -2.0, -3.0, -4.0, -6.0])


def pack_weight(w, fmt):
    k, n = w.shape
    w = f64(bf(w)).reshape(k // 32, 32, n)
    amax = np.abs(w).max(1)
    if fmt == "e4m3":
        byte = np.frexp(amax)[1] - 1 + 127 - 7
    else:
        mant, ex = np.frexp(amax / 6.0)
        byte = np.where(mant > 0.5, ex, ex - 1) + 127
    byte = np.clip(np.where(amax > 0, byte, 1), 1, 254)
    scaled = (w * np.exp2(127.0 - byte)[:, None, :]).reshape(k, n).astype(np.float32)
    by_word = np.ascontiguousarray(scaled.reshape(k // 512, 128, 4, n).transpose(0, 1, 3, 2))
    if fmt == "e4m3":
        words = by_word.astype(ml_dtypes.float8_e4m3fn).view(np.uint8)
    else:
        c = by_word.astype(ml_dtypes.float4_e2m1fn).view(np.uint8) & 0xF
        words = c[..., 0::2] | (c[..., 1::2] << 4)
    return np.ascontiguousarray(words), np.ascontiguousarray(byte.astype(np.uint8).reshape(k // 512, 16, n))


def unpack_weight(words, scales, fmt):
    g, p, n, _ = words.shape
    if fmt == "e4m3":
        vals = np.ascontiguousarray(words).view(ml_dtypes.float8_e4m3fn).astype(np.float64)
    else:
        nib = np.empty((g, p, n, 4), np.uint8)
        nib[..., 0::2] = words & 0xF
        nib[..., 1::2] = words >> 4
        vals = E2M1[nib]
    vals = vals * np.repeat(np.exp2(scales.astype(np.float64) - 127.0), 8, axis=1)[..., None]
    return vals.transpose(0, 1, 3, 2).reshape(g * 512, n)

def pack4(w):
    words, scales = pack_weight(w, "e2m1")
    return words.reshape(words.shape[0], 128, -1), scales


def unpack4(words, scales):
    return unpack_weight(words.reshape(words.shape[0], 128, -1, 2), scales, "e2m1")


B, T, C, H, W = 1, 4096, 512, 4, 512
D = C // H
HALF = D // 2
ROPE_BASE = 10000.0


def rotate_half(u):
    return np.concatenate([-u[..., HALF:], u[..., :HALF]], axis=-1)


def setup_inputs():
    s = mx_kscale(C)
    start = np.random.randint(0, T)
    inv_freq = 1.0 / (ROPE_BASE ** (np.arange(0, D, 2) / D))
    freqs = np.outer(start + np.arange(T), inv_freq)
    emb = np.concatenate([freqs, freqs], axis=-1)
    x = bf(np.random.standard_normal((B, T, C)) * s)
    words, scales = pack4(np.random.standard_normal((C, 3 * C)) * 1.25 / np.sqrt(C) / s[:, None])
    return {"x": x,
            "freqs_cos": bf(np.cos(emb)),
            "freqs_sin": bf(np.sin(emb)),
            "w_attn_words": words,
            "w_attn_scales": scales}


def reference(x, freqs_cos, freqs_sin, w_attn_words, w_attn_scales):
    qkv = mxq(f64(x), 2, "e4m3") @ unpack4(w_attn_words, w_attn_scales)
    q, k, v = np.split(qkv, 3, axis=-1)
    q = q.reshape(B, T, H, D).transpose(0, 2, 1, 3)
    k = k.reshape(B, T, H, D).transpose(0, 2, 1, 3)
    v = v.reshape(B, T, H, D).transpose(0, 2, 1, 3)
    cos = f64(freqs_cos)[None, None, :, :]
    sin = f64(freqs_sin)[None, None, :, :]
    q_rot = q * cos + rotate_half(q) * sin
    k_rot = k * cos + rotate_half(k) * sin
    return q_rot, k_rot, v

@@ -1,0 +1,181 @@
+from contextlib import ExitStack
+
+import concourse.mybir as mybir
+from concourse.masks import make_identity
+
+F32 = mybir.dt.float32
+BF16 = mybir.dt.bfloat16
+I32 = mybir.dt.int32
+U32 = mybir.dt.uint32
+U8 = mybir.dt.uint8
+FP8X4 = mybir.dt.float8_e4m3fn_x4
+FP4X4 = mybir.dt.float4_e2m1fn_x4
+MULT = mybir.AluOpType.mult
+ADD = mybir.AluOpType.add
+SUBTRACT = mybir.AluOpType.subtract
+
+P = 128
+PACK = 4
+TOKENS = 4096
+K = P * PACK
+HEADS = 4
+HEAD_DIM = 128
+HALF = HEAD_DIM // 2
+THIRD = HEADS * HEAD_DIM
+SLOTS = TOKENS // P
+GROUP = 4
+N_GROUPS = SLOTS // GROUP
+WORDS = K // 2
+Q = 0
+KEY = 1
+VALUE = 2
+
+FLOPS = 2 * TOKENS * K * 3 * THIRD
+
+
+def tile_swaattention_pa_t_kernel(
+    tc, x, freqs_cos, freqs_sin, w_attn_words, w_attn_scales, out_0, out_1, out_2
+):
+    nc = tc.nc
+    x_rows = x[0].rearrange("(p n) k -> p n k", n=SLOTS)
+    cos_rows = freqs_cos.rearrange("(p n) d -> p n d", n=SLOTS)
+    sin_rows = freqs_sin.rearrange("(p n) d -> p n d", n=SLOTS)
+    out_rows = [o[0].rearrange("h (p n) d -> p h n d", n=SLOTS) for o in (out_0, out_1, out_2)]
+
+    with ExitStack() as stack:
+        consts = stack.enter_context(tc.tile_pool(name="consts", bufs=1))
+        inputs = stack.enter_context(tc.tile_pool(name="inputs", bufs=N_GROUPS))
+        operands = stack.enter_context(tc.tile_pool(name="operands", bufs=2))
+        straights = stack.enter_context(tc.tile_pool(name="straights", bufs=4))
+        crosseds = stack.enter_context(tc.tile_pool(name="crosseds", bufs=3))
+        values = stack.enter_context(tc.tile_pool(name="values", bufs=3))
+        psum_t = stack.enter_context(tc.psum_pool(name="psum_t", bufs=2))
+        psum_qk = stack.enter_context(tc.psum_pool(name="psum_qk", bufs=4))
+        psum_v = stack.enter_context(tc.psum_pool(name="psum_v", bufs=2))
+        stack.enter_context(tc.manual_schedule())
+
+        ident = consts.tile([P, P], F32)
+        make_identity(nc, ident[:])
+
+        w_words = consts.tile([P, 2 * 3 * THIRD], U8, align_bytes=64)
+        w_scales = consts.tile([P, 3 * THIRD], U8, align_bytes=64)
+        nc.vector.memset(w_scales[:].bitcast(I32), 0)
+
+        x_tiles, cos_tiles, sin_tiles = [], [], []
+
+        def load_group(g):
+            slots = slice(g * GROUP, (g + 1) * GROUP)
+            x_g = inputs.tile([P, GROUP, K], BF16)
+            nc.sync.dma_start(out=x_g[:], in_=x_rows[:, slots, :])
+            x_tiles.append(x_g)
+            if g == 0:
+                load_weight()
+            cos_g = inputs.tile([P, GROUP, HEAD_DIM], BF16)
+            nc.sync.dma_start(out=cos_g[:], in_=cos_rows[:, slots, :])
+            cos_tiles.append(cos_g)
+            sin_g = inputs.tile([P, GROUP, HEAD_DIM], BF16)
+            nc.sync.dma_start(out=sin_g[:], in_=sin_rows[:, slots, :])
+            sin_tiles.append(sin_g)
+
+        def load_weight():
+            for quadrant in range(4):
+                nc.sync.dma_start(
+                    out=w_scales[32 * quadrant : 32 * quadrant + 4, :].bitcast(I32),
+                    in_=w_attn_scales[0, 4 * quadrant : 4 * quadrant + 4, :].bitcast(I32),
+                )
+            nc.sync.dma_start(out=w_words[:].bitcast(I32), in_=w_attn_words[0].bitcast(I32))
+
+        def transpose_group(g):
+            grouped = operands.tile([P, GROUP * P * PACK], BF16, align_bytes=64)
+            grouped_words = grouped[:].bitcast(F32).rearrange("p (s r u) -> p s r u", s=GROUP, u=2)
+            for first in range(0, GROUP, 2):
+                xt = psum_t.tile([P, 2, 2, P], F32)
+                for s in range(2):
+                    words = x_tiles[g][:, first + s, :].bitcast(F32)
+                    for u in range(2):
+                        nc.tensor.transpose(xt[:, s, u, :], words[:, u:WORDS:2], ident[:])
+                nc.scalar.copy(
+                    out=grouped_words[:, first : first + 2, :, :],
+                    in_=xt[:].rearrange("p s u r -> p s r u"),
+                )
+            swapped = inputs.tile([P, GROUP, HEAD_DIM], BF16)
+            nc.scalar.copy(out=swapped[:, :, 0:HALF], in_=sin_tiles[g][:, :, HALF:HEAD_DIM])
+            nc.scalar.copy(out=swapped[:, :, HALF:HEAD_DIM], in_=sin_tiles[g][:, :, 0:HALF])
+            return grouped, swapped
+
+        def quantise_group(grouped):
+            codes = operands.tile([P, GROUP * P], U32, align_bytes=64)
+            scales = operands.tile([P, GROUP * P], U8, align_bytes=64)
+            nc.vector.quantize_mx(out=codes[:].bitcast(FP8X4), scales=scales[:], in_=grouped[:])
+            return codes, scales
+
+        def project(bank, operand, s, third):
+            codes, scales = operand
+            tokens = slice(s * P, (s + 1) * P)
+            nc.tensor.matmul_mx(
+                out=bank[:],
+                lhsT=codes[:, tokens].bitcast(FP8X4),
+                lhsT_scale=scales[:, tokens],
+                rhs=w_words[:, 2 * third * THIRD : 2 * (third + 1) * THIRD].bitcast(FP4X4),
+                rhs_scale=w_scales[:, third * THIRD : (third + 1) * THIRD],
+                start=True,
+                stop=True,
+            )
+
+        def over_heads(table, s):
+            return table[:, s, :].unsqueeze(1).to_broadcast([P, HEADS, HEAD_DIM])
+
+        def multiply(g, third, operand, swapped):
+            straight = straights.tile([P, HEADS, GROUP, HEAD_DIM], F32)
+            crossed = crosseds.tile([P, HEADS, GROUP, HEAD_DIM], F32)
+            for s in range(GROUP):
+                bank = psum_qk.tile([P, THIRD], F32)
+                project(bank, operand, s, third)
+                by_head = bank[:].rearrange("p (h d) -> p h d", h=HEADS)
+                nc.vector.tensor_tensor(
+                    out=straight[:, :, s, :], in0=by_head, in1=over_heads(cos_tiles[g], s), op=MULT
+                )
+                nc.vector.tensor_tensor(
+                    out=crossed[:, :, s, :], in0=by_head, in1=over_heads(swapped, s), op=MULT
+                )
+            return straight, crossed
+
+        def combine_and_store(g, third, straight, crossed):
+            a = straight[:].rearrange("p h s d -> p (h s) d")
+            b = crossed[:].rearrange("p h s d -> p (h s) d")
+            low, high = slice(0, HALF), slice(HALF, HEAD_DIM)
+            nc.gpsimd.tensor_tensor(out=a[:, :, low], in0=a[:, :, low], in1=b[:, :, high], op=SUBTRACT)
+            nc.gpsimd.tensor_tensor(out=a[:, :, high], in0=a[:, :, high], in1=b[:, :, low], op=ADD)
+            nc.sync.dma_start(
+                out=out_rows[third][:, :, g * GROUP : (g + 1) * GROUP, :], in_=straight[:]
+            )
+
+        def copy_and_store_v(g, operand):
+            v_rows = values.tile([P, HEADS, GROUP, HEAD_DIM], F32)
+            for s in range(GROUP):
+                bank = psum_v.tile([P, THIRD], F32)
+                project(bank, operand, s, VALUE)
+                nc.scalar.copy(
+                    out=v_rows[:, :, s, :], in_=bank[:].rearrange("p (h d) -> p h d", h=HEADS)
+                )
+            nc.sync.dma_start(
+                out=out_rows[VALUE][:, :, g * GROUP : (g + 1) * GROUP, :], in_=v_rows[:]
+            )
+
+        for g in range(N_GROUPS):
+            load_group(g)
+
+        grouped, swapped = transpose_group(0)
+        operand = quantise_group(grouped)
+        for g in range(N_GROUPS):
+            last = g == N_GROUPS - 1
+            straight, crossed = multiply(g, Q, operand, swapped)
+            combine_and_store(g, Q, straight, crossed)
+            if not last:
+                grouped, next_swapped = transpose_group(g + 1)
+                next_operand = quantise_group(grouped)
+            straight, crossed = multiply(g, KEY, operand, swapped)
+            copy_and_store_v(g, operand)
+            combine_and_store(g, KEY, straight, crossed)
+            if not last:
+                operand, swapped = next_operand, next_swapped

@@ -140,12 +140,12 @@ def tile_swaattention_pa_t_kernel(
                 )
             return straight, crossed
 
-        def combine_and_store(g, third, straight, crossed):
+        def combine_and_store(g, third, straight, crossed, adder):
             a = straight[:].rearrange("p h s d -> p (h s) d")
             b = crossed[:].rearrange("p h s d -> p (h s) d")
             low, high = slice(0, HALF), slice(HALF, HEAD_DIM)
-            nc.gpsimd.tensor_tensor(out=a[:, :, low], in0=a[:, :, low], in1=b[:, :, high], op=SUBTRACT)
-            nc.gpsimd.tensor_tensor(out=a[:, :, high], in0=a[:, :, high], in1=b[:, :, low], op=ADD)
+            adder.tensor_tensor(out=a[:, :, low], in0=a[:, :, low], in1=b[:, :, high], op=SUBTRACT)
+            adder.tensor_tensor(out=a[:, :, high], in0=a[:, :, high], in1=b[:, :, low], op=ADD)
             nc.sync.dma_start(
                 out=out_rows[third][:, :, g * GROUP : (g + 1) * GROUP, :], in_=straight[:]
             )
@@ -158,7 +158,7 @@ def tile_swaattention_pa_t_kernel(
                 nc.scalar.copy(
                     out=v_rows[:, :, s, :], in_=bank[:].rearrange("p (h d) -> p h d", h=HEADS)
                 )
-            nc.sync.dma_start(
+            nc.scalar.dma_start(
                 out=out_rows[VALUE][:, :, g * GROUP : (g + 1) * GROUP, :], in_=v_rows[:]
             )
 
@@ -170,12 +170,12 @@ def tile_swaattention_pa_t_kernel(
         for g in range(N_GROUPS):
             last = g == N_GROUPS - 1
             straight, crossed = multiply(g, Q, operand, swapped)
-            combine_and_store(g, Q, straight, crossed)
+            combine_and_store(g, Q, straight, crossed, nc.gpsimd)
             if not last:
                 grouped, next_swapped = transpose_group(g + 1)
                 next_operand = quantise_group(grouped)
             straight, crossed = multiply(g, KEY, operand, swapped)
             copy_and_store_v(g, operand)
-            combine_and_store(g, KEY, straight, crossed)
+            combine_and_store(g, KEY, straight, crossed, nc.vector if last else nc.gpsimd)
             if not last:
                 operand, swapped = next_operand, next_swapped

@@ -12,7 +12,6 @@ FP8X4 = mybir.dt.float8_e4m3fn_x4
 FP4X4 = mybir.dt.float4_e2m1fn_x4
 MULT = mybir.AluOpType.mult
 ADD = mybir.AluOpType.add
-SUBTRACT = mybir.AluOpType.subtract
 
 P = 128
 PACK = 4
@@ -46,22 +45,32 @@ def tile_swaattention_pa_t_kernel(
         consts = stack.enter_context(tc.tile_pool(name="consts", bufs=1))
         inputs = stack.enter_context(tc.tile_pool(name="inputs", bufs=N_GROUPS))
         operands = stack.enter_context(tc.tile_pool(name="operands", bufs=2))
-        straights = stack.enter_context(tc.tile_pool(name="straights", bufs=4))
+        tables = stack.enter_context(tc.tile_pool(name="tables", bufs=3))
+        straights = stack.enter_context(tc.tile_pool(name="straights", bufs=3))
         crosseds = stack.enter_context(tc.tile_pool(name="crosseds", bufs=3))
         values = stack.enter_context(tc.tile_pool(name="values", bufs=3))
-        psum_t = stack.enter_context(tc.psum_pool(name="psum_t", bufs=2))
-        psum_qk = stack.enter_context(tc.psum_pool(name="psum_qk", bufs=4))
-        psum_v = stack.enter_context(tc.psum_pool(name="psum_v", bufs=2))
+        keys = stack.enter_context(tc.tile_pool(name="keys", bufs=3))
+        products = stack.enter_context(tc.tile_pool(name="products", bufs=6))
+        psum_vec = stack.enter_context(tc.psum_pool(name="psum_vec", bufs=4))
+        psum_act = stack.enter_context(tc.psum_pool(name="psum_act", bufs=2))
+        psum_prep = stack.enter_context(tc.psum_pool(name="psum_prep", bufs=2))
         stack.enter_context(tc.manual_schedule())
 
         ident = consts.tile([P, P], F32)
         make_identity(nc, ident[:])
+        ident_bf = consts.tile([P, P], BF16)
+        make_identity(nc, ident_bf[:])
+        perm = consts.tile([P, P], F32)
+        nc.vector.tensor_copy(out=perm[:, 0:HALF], in_=ident[:, HALF:P])
+        nc.vector.tensor_copy(out=perm[:, HALF:P], in_=ident[:, 0:HALF])
 
         w_words = consts.tile([P, 2 * 3 * THIRD], U8, align_bytes=64)
         w_scales = consts.tile([P, 3 * THIRD], U8, align_bytes=64)
         nc.vector.memset(w_scales[:].bitcast(I32), 0)
 
         x_tiles, cos_tiles, sin_tiles = [], [], []
+        grouped_of, operand_of, swapped_of, table_of = {}, {}, {}, {}
+        bank_of, product_of, straight_of, crossed_of, k_rows_of, v_rows_of = {}, {}, {}, {}, {}, {}
 
         def load_group(g):
             slots = slice(g * GROUP, (g + 1) * GROUP)
@@ -85,32 +94,48 @@ def tile_swaattention_pa_t_kernel(
                 )
             nc.sync.dma_start(out=w_words[:].bitcast(I32), in_=w_attn_words[0].bitcast(I32))
 
-        def transpose_group(g):
-            grouped = operands.tile([P, GROUP * P * PACK], BF16, align_bytes=64)
-            grouped_words = grouped[:].bitcast(F32).rearrange("p (s r u) -> p s r u", s=GROUP, u=2)
-            for first in range(0, GROUP, 2):
-                xt = psum_t.tile([P, 2, 2, P], F32)
-                for s in range(2):
-                    words = x_tiles[g][:, first + s, :].bitcast(F32)
-                    for u in range(2):
-                        nc.tensor.transpose(xt[:, s, u, :], words[:, u:WORDS:2], ident[:])
-                nc.scalar.copy(
-                    out=grouped_words[:, first : first + 2, :, :],
-                    in_=xt[:].rearrange("p s u r -> p s r u"),
-                )
+        def prep_x(g, half):
+            if half == 0:
+                grouped = operands.tile([P, GROUP * P * PACK], BF16, align_bytes=64)
+                grouped_of[g] = grouped
+            grouped_words = (
+                grouped_of[g][:].bitcast(F32).rearrange("p (s r u) -> p s r u", s=GROUP, u=2)
+            )
+            first = 2 * half
+            xt = psum_prep.tile([P, 2, 2, P], F32, name="prep")
+            for s in range(2):
+                words = x_tiles[g][:, first + s, :].bitcast(F32)
+                for u in range(2):
+                    nc.tensor.transpose(xt[:, s, u, :], words[:, u:WORDS:2], ident[:])
+            nc.scalar.copy(
+                out=grouped_words[:, first : first + 2, :, :],
+                in_=xt[:].rearrange("p s u r -> p s r u"),
+            )
+
+        def swap_sin(g):
             swapped = inputs.tile([P, GROUP, HEAD_DIM], BF16)
             nc.scalar.copy(out=swapped[:, :, 0:HALF], in_=sin_tiles[g][:, :, HALF:HEAD_DIM])
-            nc.scalar.copy(out=swapped[:, :, HALF:HEAD_DIM], in_=sin_tiles[g][:, :, 0:HALF])
-            return grouped, swapped
+            nc.scalar.mul(out=swapped[:, :, HALF:HEAD_DIM], in_=sin_tiles[g][:, :, 0:HALF], mul=-1.0)
+            swapped_of[g] = swapped
 
-        def quantise_group(grouped):
+        def prep_tables(g):
+            tab_ps = psum_prep.tile([P, 2, GROUP * P], BF16, name="prep")
+            for s in range(GROUP):
+                nc.tensor.transpose(tab_ps[:, 0, s * P : (s + 1) * P], cos_tiles[g][:, s, :], ident_bf[:])
+            for s in range(GROUP):
+                nc.tensor.transpose(tab_ps[:, 1, s * P : (s + 1) * P], swapped_of[g][:, s, :], ident_bf[:])
+            table = tables.tile([P, 2, GROUP * P], BF16)
+            nc.scalar.copy(out=table[:], in_=tab_ps[:])
+            table_of[g] = table
+
+        def quantise(g):
             codes = operands.tile([P, GROUP * P], U32, align_bytes=64)
             scales = operands.tile([P, GROUP * P], U8, align_bytes=64)
-            nc.vector.quantize_mx(out=codes[:].bitcast(FP8X4), scales=scales[:], in_=grouped[:])
-            return codes, scales
+            nc.vector.quantize_mx(out=codes[:].bitcast(FP8X4), scales=scales[:], in_=grouped_of[g][:])
+            operand_of[g] = (codes, scales)
 
-        def project(bank, operand, s, third):
-            codes, scales = operand
+        def project(bank, g, s, third):
+            codes, scales = operand_of[g]
             tokens = slice(s * P, (s + 1) * P)
             nc.tensor.matmul_mx(
                 out=bank[:],
@@ -122,60 +147,178 @@ def tile_swaattention_pa_t_kernel(
                 stop=True,
             )
 
+        def mx_q(g, s):
+            bank = psum_vec.tile([P, THIRD], F32, name="bank")
+            project(bank, g, s, Q)
+            bank_of[(Q, g, s)] = bank
+
+        def mx_k(g, h):
+            codes, scales = operand_of[g]
+            first = KEY * THIRD + h * HEAD_DIM
+            bank = psum_vec.tile([P, GROUP * P], F32, name="bank")
+            nc.tensor.matmul_mx(
+                out=bank[:],
+                lhsT=w_words[:, 2 * first : 2 * (first + HEAD_DIM)].bitcast(FP4X4),
+                lhsT_scale=w_scales[:, first : first + HEAD_DIM],
+                rhs=codes[:].bitcast(FP8X4),
+                rhs_scale=scales[:],
+                start=True,
+                stop=True,
+            )
+            bank_of[(KEY, g, h)] = bank
+
         def over_heads(table, s):
             return table[:, s, :].unsqueeze(1).to_broadcast([P, HEADS, HEAD_DIM])
 
-        def multiply(g, third, operand, swapped):
-            straight = straights.tile([P, HEADS, GROUP, HEAD_DIM], F32)
-            crossed = crosseds.tile([P, HEADS, GROUP, HEAD_DIM], F32)
-            for s in range(GROUP):
-                bank = psum_qk.tile([P, THIRD], F32)
-                project(bank, operand, s, third)
-                by_head = bank[:].rearrange("p (h d) -> p h d", h=HEADS)
-                nc.vector.tensor_tensor(
-                    out=straight[:, :, s, :], in0=by_head, in1=over_heads(cos_tiles[g], s), op=MULT
-                )
-                nc.vector.tensor_tensor(
-                    out=crossed[:, :, s, :], in0=by_head, in1=over_heads(swapped, s), op=MULT
-                )
-            return straight, crossed
-
-        def combine_and_store(g, third, straight, crossed, adder):
-            a = straight[:].rearrange("p h s d -> p (h s) d")
-            b = crossed[:].rearrange("p h s d -> p (h s) d")
-            low, high = slice(0, HALF), slice(HALF, HEAD_DIM)
-            adder.tensor_tensor(out=a[:, :, low], in0=a[:, :, low], in1=b[:, :, high], op=SUBTRACT)
-            adder.tensor_tensor(out=a[:, :, high], in0=a[:, :, high], in1=b[:, :, low], op=ADD)
-            nc.sync.dma_start(
-                out=out_rows[third][:, :, g * GROUP : (g + 1) * GROUP, :], in_=straight[:]
+        def mult_q_straight(g, s):
+            if s == 0:
+                straight = straights.tile([P, HEADS, GROUP, HEAD_DIM], F32)
+                straight_of[g] = straight
+                crossed = crosseds.tile([P, HEADS, GROUP, HEAD_DIM], F32)
+                crossed_of[g] = crossed
+            by_head = bank_of[(Q, g, s)][:].rearrange("p (h d) -> p h d", h=HEADS)
+            nc.vector.tensor_tensor(
+                out=straight_of[g][:, :, s, :], in0=by_head, in1=over_heads(cos_tiles[g], s), op=MULT
             )
 
-        def copy_and_store_v(g, operand):
-            v_rows = values.tile([P, HEADS, GROUP, HEAD_DIM], F32)
+        def mult_q_crossed(g, s):
+            by_head = bank_of[(Q, g, s)][:].rearrange("p (h d) -> p h d", h=HEADS)
+            nc.vector.tensor_tensor(
+                out=crossed_of[g][:, :, s, :], in0=by_head, in1=over_heads(swapped_of[g], s), op=MULT
+            )
+
+        def add_q(g, first, count):
+            a = straight_of[g][:, :, first : first + count, :]
+            b = crossed_of[g][:, :, first : first + count, :]
+            low, high = slice(0, HALF), slice(HALF, HEAD_DIM)
+            nc.gpsimd.tensor_tensor(
+                out=a[:, :, :, low], in0=a[:, :, :, low], in1=b[:, :, :, high], op=ADD
+            )
+            nc.gpsimd.tensor_tensor(
+                out=a[:, :, :, high], in0=a[:, :, :, high], in1=b[:, :, :, low], op=ADD
+            )
+            nc.sync.dma_start(
+                out=out_rows[Q][:, :, g * GROUP + first : g * GROUP + first + count, :], in_=a
+            )
+
+        def mult_k(g, h):
+            bank = bank_of[(KEY, g, h)]
+            straight_t = products.tile([P, GROUP * P], F32)
+            crossed_t = products.tile([P, GROUP * P], F32)
+            nc.vector.tensor_tensor(out=straight_t[:], in0=bank[:], in1=table_of[g][:, 0, :], op=MULT)
+            nc.vector.tensor_tensor(out=crossed_t[:], in0=bank[:], in1=table_of[g][:, 1, :], op=MULT)
+            product_of[(g, h)] = (straight_t, crossed_t)
+
+        def back_k(g, h):
+            if h == 0:
+                k_rows = keys.tile([P, HEADS, GROUP, HEAD_DIM], F32)
+                k_rows_of[g] = k_rows
+            straight_t, crossed_t = product_of[(g, h)]
+            summed = psum_act.tile([P, GROUP, HEAD_DIM], F32, name="evac")
             for s in range(GROUP):
-                bank = psum_v.tile([P, THIRD], F32)
-                project(bank, operand, s, VALUE)
-                nc.scalar.copy(
-                    out=v_rows[:, :, s, :], in_=bank[:].rearrange("p (h d) -> p h d", h=HEADS)
+                tokens = slice(s * P, (s + 1) * P)
+                nc.tensor.matmul(
+                    out=summed[:, s, :], lhsT=straight_t[:, tokens], rhs=ident[:],
+                    is_transpose=True, start=True, stop=False,
                 )
+                nc.tensor.matmul(
+                    out=summed[:, s, :], lhsT=crossed_t[:, tokens], rhs=perm[:],
+                    is_transpose=True, start=False, stop=True,
+                )
+            nc.scalar.copy(out=k_rows_of[g][:, h, :, :], in_=summed[:])
+
+        def store_k(g, first, count):
+            nc.sync.dma_start(
+                out=out_rows[KEY][:, first : first + count, g * GROUP : (g + 1) * GROUP, :],
+                in_=k_rows_of[g][:, first : first + count, :, :],
+            )
+
+        def mx_v(g, s):
+            if s == 0:
+                v_rows = values.tile([P, HEADS, GROUP, HEAD_DIM], F32)
+                v_rows_of[g] = v_rows
+            bank = psum_act.tile([P, THIRD], F32, name="evac")
+            project(bank, g, s, VALUE)
+            nc.scalar.copy(
+                out=v_rows_of[g][:, :, s, :], in_=bank[:].rearrange("p (h d) -> p h d", h=HEADS)
+            )
+
+        def store_v(g):
             nc.scalar.dma_start(
-                out=out_rows[VALUE][:, :, g * GROUP : (g + 1) * GROUP, :], in_=v_rows[:]
+                out=out_rows[VALUE][:, :, g * GROUP : (g + 1) * GROUP, :], in_=v_rows_of[g][:]
             )
 
         for g in range(N_GROUPS):
             load_group(g)
 
-        grouped, swapped = transpose_group(0)
-        operand = quantise_group(grouped)
+        prep_x(0, 0)
+        prep_x(0, 1)
+        quantise(0)
+        for s in range(GROUP):
+            mx_q(0, s)
+        prep_x(1, 0)
+        prep_x(1, 1)
+        swap_sin(0)
+        prep_tables(0)
+        swap_sin(1)
+
         for g in range(N_GROUPS):
-            last = g == N_GROUPS - 1
-            straight, crossed = multiply(g, Q, operand, swapped)
-            combine_and_store(g, Q, straight, crossed, nc.gpsimd)
-            if not last:
-                grouped, next_swapped = transpose_group(g + 1)
-                next_operand = quantise_group(grouped)
-            straight, crossed = multiply(g, KEY, operand, swapped)
-            copy_and_store_v(g, operand)
-            combine_and_store(g, KEY, straight, crossed, nc.vector if last else nc.gpsimd)
-            if not last:
-                operand, swapped = next_operand, next_swapped
+            has_next = g + 1 < N_GROUPS
+            last = not has_next
+            mult_q_straight(g, 0)
+            mult_q_crossed(g, 0)
+            mult_q_straight(g, 1)
+            mult_q_crossed(g, 1)
+            if last:
+                add_q(g, 0, 2)
+            mult_q_straight(g, 2)
+            mult_q_crossed(g, 2)
+            if has_next:
+                prep_tables(g + 1)
+            if g > 0:
+                back_k(g - 1, 2)
+                back_k(g - 1, 3)
+                store_k(g - 1, 0, HEADS)
+            mult_q_straight(g, 3)
+            if has_next:
+                quantise(g + 1)
+            mult_q_crossed(g, 3)
+            if last:
+                add_q(g, 2, 2)
+            else:
+                add_q(g, 0, GROUP)
+            mx_k(g, 0)
+            mx_k(g, 1)
+            mx_k(g, 2)
+            mx_v(g, 0)
+            mx_v(g, 1)
+            if last:
+                mx_v(g, 2)
+                mx_v(g, 3)
+                store_v(g)
+            mx_k(g, 3)
+            mult_k(g, 0)
+            mult_k(g, 1)
+            if g + 2 < N_GROUPS:
+                prep_x(g + 2, 0)
+                prep_x(g + 2, 1)
+            back_k(g, 0)
+            back_k(g, 1)
+            if last:
+                store_k(g, 0, 2)
+            mult_k(g, 2)
+            if last:
+                back_k(g, 2)
+            mult_k(g, 3)
+            if has_next:
+                mx_q(g + 1, 0)
+                mx_q(g + 1, 1)
+                mx_q(g + 1, 2)
+                mx_v(g, 2)
+                mx_v(g, 3)
+                mx_q(g + 1, 3)
+                store_v(g)
+            if g + 2 < N_GROUPS:
+                swap_sin(g + 2)
+        back_k(N_GROUPS - 1, 3)
+        store_k(N_GROUPS - 1, 2, 2)

@@ -51,6 +51,7 @@ def tile_swaattention_pa_t_kernel(
         values = stack.enter_context(tc.tile_pool(name="values", bufs=3))
         keys = stack.enter_context(tc.tile_pool(name="keys", bufs=3))
         products = stack.enter_context(tc.tile_pool(name="products", bufs=6))
+        copies = stack.enter_context(tc.tile_pool(name="copies", bufs=2))
         psum_vec = stack.enter_context(tc.psum_pool(name="psum_vec", bufs=4))
         psum_act = stack.enter_context(tc.psum_pool(name="psum_act", bufs=2))
         psum_prep = stack.enter_context(tc.psum_pool(name="psum_prep", bufs=2))
@@ -71,14 +72,16 @@ def tile_swaattention_pa_t_kernel(
         x_tiles, cos_tiles, sin_tiles = [], [], []
         grouped_of, operand_of, swapped_of, table_of = {}, {}, {}, {}
         bank_of, product_of, straight_of, crossed_of, k_rows_of, v_rows_of = {}, {}, {}, {}, {}, {}
+        copy_of = {}
 
-        def load_group(g):
+        def load_x(g):
             slots = slice(g * GROUP, (g + 1) * GROUP)
             x_g = inputs.tile([P, GROUP, K], BF16)
             nc.sync.dma_start(out=x_g[:], in_=x_rows[:, slots, :])
             x_tiles.append(x_g)
-            if g == 0:
-                load_weight()
+
+        def load_tables(g):
+            slots = slice(g * GROUP, (g + 1) * GROUP)
             cos_g = inputs.tile([P, GROUP, HEAD_DIM], BF16)
             nc.sync.dma_start(out=cos_g[:], in_=cos_rows[:, slots, :])
             cos_tiles.append(cos_g)
@@ -170,12 +173,28 @@ def tile_swaattention_pa_t_kernel(
         def over_heads(table, s):
             return table[:, s, :].unsqueeze(1).to_broadcast([P, HEADS, HEAD_DIM])
 
+        def mx_q_copy(g):
+            bank = psum_act.tile([P, THIRD], F32, name="evac")
+            project(bank, g, GROUP - 1, Q)
+            q_copy = copies.tile([P, THIRD], F32)
+            nc.scalar.copy(out=q_copy[:], in_=bank[:])
+            copy_of[g] = q_copy
+
+        def mult_q_gpsimd(g):
+            straight = straights.tile([P, HEADS, GROUP, HEAD_DIM], F32)
+            straight_of[g] = straight
+            crossed = crosseds.tile([P, HEADS, GROUP, HEAD_DIM], F32)
+            crossed_of[g] = crossed
+            s = GROUP - 1
+            by_head = copy_of[g][:].rearrange("p (h d) -> p h d", h=HEADS)
+            nc.gpsimd.tensor_tensor(
+                out=straight[:, :, s, :], in0=by_head, in1=over_heads(cos_tiles[g], s), op=MULT
+            )
+            nc.gpsimd.tensor_tensor(
+                out=crossed[:, :, s, :], in0=by_head, in1=over_heads(swapped_of[g], s), op=MULT
+            )
+
         def mult_q_straight(g, s):
-            if s == 0:
-                straight = straights.tile([P, HEADS, GROUP, HEAD_DIM], F32)
-                straight_of[g] = straight
-                crossed = crosseds.tile([P, HEADS, GROUP, HEAD_DIM], F32)
-                crossed_of[g] = crossed
             by_head = bank_of[(Q, g, s)][:].rearrange("p (h d) -> p h d", h=HEADS)
             nc.vector.tensor_tensor(
                 out=straight_of[g][:, :, s, :], in0=by_head, in1=over_heads(cos_tiles[g], s), op=MULT
@@ -248,23 +267,33 @@ def tile_swaattention_pa_t_kernel(
                 out=out_rows[VALUE][:, :, g * GROUP : (g + 1) * GROUP, :], in_=v_rows_of[g][:]
             )
 
-        for g in range(N_GROUPS):
-            load_group(g)
+        load_x(0)
+        load_x(1)
+        load_weight()
+        load_tables(0)
+        load_tables(1)
+        for g in range(2, N_GROUPS):
+            load_x(g)
+            load_tables(g)
 
         prep_x(0, 0)
         prep_x(0, 1)
         quantise(0)
-        for s in range(GROUP):
-            mx_q(0, s)
+        swap_sin(0)
         prep_x(1, 0)
         prep_x(1, 1)
-        swap_sin(0)
-        prep_tables(0)
+        mx_q(0, 0)
+        mx_q(0, 1)
+        mx_q(0, 2)
+        mx_k(0, 0)
+        mx_q_copy(0)
         swap_sin(1)
+        prep_tables(0)
 
         for g in range(N_GROUPS):
             has_next = g + 1 < N_GROUPS
             last = not has_next
+            mult_q_gpsimd(g)
             mult_q_straight(g, 0)
             mult_q_crossed(g, 0)
             mult_q_straight(g, 1)
@@ -272,32 +301,35 @@ def tile_swaattention_pa_t_kernel(
             if last:
                 add_q(g, 0, 2)
             mult_q_straight(g, 2)
-            mult_q_crossed(g, 2)
             if has_next:
                 prep_tables(g + 1)
             if g > 0:
                 back_k(g - 1, 2)
                 back_k(g - 1, 3)
                 store_k(g - 1, 0, HEADS)
-            mult_q_straight(g, 3)
+            if g + 2 < N_GROUPS:
+                swap_sin(g + 2)
             if has_next:
                 quantise(g + 1)
-            mult_q_crossed(g, 3)
+            mult_q_crossed(g, 2)
             if last:
                 add_q(g, 2, 2)
             else:
                 add_q(g, 0, GROUP)
-            mx_k(g, 0)
             mx_k(g, 1)
             mx_k(g, 2)
+            mx_k(g, 3)
+            if has_next:
+                mx_q_copy(g + 1)
             mx_v(g, 0)
             mx_v(g, 1)
             if last:
                 mx_v(g, 2)
                 mx_v(g, 3)
                 store_v(g)
-            mx_k(g, 3)
             mult_k(g, 0)
+            if has_next:
+                mx_q(g + 1, 0)
             mult_k(g, 1)
             if g + 2 < N_GROUPS:
                 prep_x(g + 2, 0)
@@ -311,14 +343,11 @@ def tile_swaattention_pa_t_kernel(
                 back_k(g, 2)
             mult_k(g, 3)
             if has_next:
-                mx_q(g + 1, 0)
                 mx_q(g + 1, 1)
                 mx_q(g + 1, 2)
+                mx_k(g + 1, 0)
                 mx_v(g, 2)
                 mx_v(g, 3)
-                mx_q(g + 1, 3)
                 store_v(g)
-            if g + 2 < N_GROUPS:
-                swap_sin(g + 2)
         back_k(N_GROUPS - 1, 3)
         store_k(N_GROUPS - 1, 2, 2)

@@ -46,8 +46,7 @@ def tile_swaattention_pa_t_kernel(
         inputs = stack.enter_context(tc.tile_pool(name="inputs", bufs=N_GROUPS))
         operands = stack.enter_context(tc.tile_pool(name="operands", bufs=2))
         tables = stack.enter_context(tc.tile_pool(name="tables", bufs=3))
-        straights = stack.enter_context(tc.tile_pool(name="straights", bufs=3))
-        crosseds = stack.enter_context(tc.tile_pool(name="crosseds", bufs=3))
+        pairs = stack.enter_context(tc.tile_pool(name="pairs", bufs=3))
         values = stack.enter_context(tc.tile_pool(name="values", bufs=3))
         keys = stack.enter_context(tc.tile_pool(name="keys", bufs=3))
         products = stack.enter_context(tc.tile_pool(name="products", bufs=6))
@@ -69,8 +68,8 @@ def tile_swaattention_pa_t_kernel(
         w_scales = consts.tile([P, 3 * THIRD], U8, align_bytes=64)
         nc.vector.memset(w_scales[:].bitcast(I32), 0)
 
-        x_tiles, cos_tiles, sin_tiles = [], [], []
-        grouped_of, operand_of, swapped_of, table_of = {}, {}, {}, {}
+        x_tiles, factor_tiles, sin_tiles = [], [], []
+        grouped_of, operand_of, table_of = {}, {}, {}
         bank_of, product_of, straight_of, crossed_of, k_rows_of, v_rows_of = {}, {}, {}, {}, {}, {}
         copy_of = {}
 
@@ -82,9 +81,9 @@ def tile_swaattention_pa_t_kernel(
 
         def load_tables(g):
             slots = slice(g * GROUP, (g + 1) * GROUP)
-            cos_g = inputs.tile([P, GROUP, HEAD_DIM], BF16)
-            nc.sync.dma_start(out=cos_g[:], in_=cos_rows[:, slots, :])
-            cos_tiles.append(cos_g)
+            factors = inputs.tile([P, 2, GROUP, HEAD_DIM], BF16)
+            nc.sync.dma_start(out=factors[:, 0, :, :], in_=cos_rows[:, slots, :])
+            factor_tiles.append(factors)
             sin_g = inputs.tile([P, GROUP, HEAD_DIM], BF16)
             nc.sync.dma_start(out=sin_g[:], in_=sin_rows[:, slots, :])
             sin_tiles.append(sin_g)
@@ -116,17 +115,17 @@ def tile_swaattention_pa_t_kernel(
             )
 
         def swap_sin(g):
-            swapped = inputs.tile([P, GROUP, HEAD_DIM], BF16)
+            swapped = factor_tiles[g][:, 1, :, :]
             nc.scalar.copy(out=swapped[:, :, 0:HALF], in_=sin_tiles[g][:, :, HALF:HEAD_DIM])
             nc.scalar.mul(out=swapped[:, :, HALF:HEAD_DIM], in_=sin_tiles[g][:, :, 0:HALF], mul=-1.0)
-            swapped_of[g] = swapped
 
         def prep_tables(g):
             tab_ps = psum_prep.tile([P, 2, GROUP * P], BF16, name="prep")
-            for s in range(GROUP):
-                nc.tensor.transpose(tab_ps[:, 0, s * P : (s + 1) * P], cos_tiles[g][:, s, :], ident_bf[:])
-            for s in range(GROUP):
-                nc.tensor.transpose(tab_ps[:, 1, s * P : (s + 1) * P], swapped_of[g][:, s, :], ident_bf[:])
+            for which in range(2):
+                for s in range(GROUP):
+                    nc.tensor.transpose(
+                        tab_ps[:, which, s * P : (s + 1) * P], factor_tiles[g][:, which, s, :], ident_bf[:]
+                    )
             table = tables.tile([P, 2, GROUP * P], BF16)
             nc.scalar.copy(out=table[:], in_=tab_ps[:])
             table_of[g] = table
@@ -170,8 +169,8 @@ def tile_swaattention_pa_t_kernel(
             )
             bank_of[(KEY, g, h)] = bank
 
-        def over_heads(table, s):
-            return table[:, s, :].unsqueeze(1).to_broadcast([P, HEADS, HEAD_DIM])
+        def over_heads(g, which, s):
+            return factor_tiles[g][:, which, s, :].unsqueeze(1).to_broadcast([P, HEADS, HEAD_DIM])
 
         def mx_q_copy(g):
             bank = psum_act.tile([P, THIRD], F32, name="evac")
@@ -181,41 +180,49 @@ def tile_swaattention_pa_t_kernel(
             copy_of[g] = q_copy
 
         def mult_q_gpsimd(g):
-            straight = straights.tile([P, HEADS, GROUP, HEAD_DIM], F32)
-            straight_of[g] = straight
-            crossed = crosseds.tile([P, HEADS, GROUP, HEAD_DIM], F32)
-            crossed_of[g] = crossed
+            pair = pairs.tile([P, 2, HEADS, GROUP, HEAD_DIM], F32)
+            straight_of[g] = pair[:, 0, :, :, :]
+            crossed_of[g] = pair[:, 1, :, :, :]
             s = GROUP - 1
+            shape = [P, 2, HEADS, HEAD_DIM]
             by_head = copy_of[g][:].rearrange("p (h d) -> p h d", h=HEADS)
             nc.gpsimd.tensor_tensor(
-                out=straight[:, :, s, :], in0=by_head, in1=over_heads(cos_tiles[g], s), op=MULT
-            )
-            nc.gpsimd.tensor_tensor(
-                out=crossed[:, :, s, :], in0=by_head, in1=over_heads(swapped_of[g], s), op=MULT
+                out=pair[:, :, :, s, :],
+                in0=by_head.unsqueeze(1).to_broadcast(shape),
+                in1=factor_tiles[g][:, :, s, :].unsqueeze(2).to_broadcast(shape),
+                op=MULT,
             )
 
         def mult_q_straight(g, s):
             by_head = bank_of[(Q, g, s)][:].rearrange("p (h d) -> p h d", h=HEADS)
             nc.vector.tensor_tensor(
-                out=straight_of[g][:, :, s, :], in0=by_head, in1=over_heads(cos_tiles[g], s), op=MULT
+                out=straight_of[g][:, :, s, :], in0=by_head, in1=over_heads(g, 0, s), op=MULT
             )
 
         def mult_q_crossed(g, s):
             by_head = bank_of[(Q, g, s)][:].rearrange("p (h d) -> p h d", h=HEADS)
             nc.vector.tensor_tensor(
-                out=crossed_of[g][:, :, s, :], in0=by_head, in1=over_heads(swapped_of[g], s), op=MULT
+                out=crossed_of[g][:, :, s, :], in0=by_head, in1=over_heads(g, 1, s), op=MULT
             )
 
         def add_q(g, first, count):
             a = straight_of[g][:, :, first : first + count, :]
             b = crossed_of[g][:, :, first : first + count, :]
-            low, high = slice(0, HALF), slice(HALF, HEAD_DIM)
-            nc.gpsimd.tensor_tensor(
-                out=a[:, :, :, low], in0=a[:, :, :, low], in1=b[:, :, :, high], op=ADD
-            )
-            nc.gpsimd.tensor_tensor(
-                out=a[:, :, :, high], in0=a[:, :, :, high], in1=b[:, :, :, low], op=ADD
-            )
+            if count == GROUP:
+                halves = "p h s (e c) -> p (h s) e c"
+                a_halves = a.rearrange(halves, e=2)
+                b_halves = b.rearrange(halves, e=2)
+                nc.gpsimd.tensor_tensor(
+                    out=a_halves, in0=a_halves, in1=b_halves[:, :, ::-1, :], op=ADD
+                )
+            else:
+                low, high = slice(0, HALF), slice(HALF, HEAD_DIM)
+                nc.gpsimd.tensor_tensor(
+                    out=a[:, :, :, low], in0=a[:, :, :, low], in1=b[:, :, :, high], op=ADD
+                )
+                nc.gpsimd.tensor_tensor(
+                    out=a[:, :, :, high], in0=a[:, :, :, high], in1=b[:, :, :, low], op=ADD
+                )
             nc.sync.dma_start(
                 out=out_rows[Q][:, :, g * GROUP + first : g * GROUP + first + count, :], in_=a
             )

@@ -52,8 +52,7 @@ def tile_swaattention_pa_t_kernel(
         products = stack.enter_context(tc.tile_pool(name="products", bufs=6))
         copies = stack.enter_context(tc.tile_pool(name="copies", bufs=2))
         psum_vec = stack.enter_context(tc.psum_pool(name="psum_vec", bufs=4))
-        psum_act = stack.enter_context(tc.psum_pool(name="psum_act", bufs=2))
-        psum_prep = stack.enter_context(tc.psum_pool(name="psum_prep", bufs=2))
+        psum_act = stack.enter_context(tc.psum_pool(name="psum_act", bufs=4))
         stack.enter_context(tc.manual_schedule())
 
         ident = consts.tile([P, P], F32)
@@ -104,7 +103,7 @@ def tile_swaattention_pa_t_kernel(
                 grouped_of[g][:].bitcast(F32).rearrange("p (s r u) -> p s r u", s=GROUP, u=2)
             )
             first = 2 * half
-            xt = psum_prep.tile([P, 2, 2, P], F32, name="prep")
+            xt = psum_act.tile([P, 2, 2, P], F32, name="evac")
             for s in range(2):
                 words = x_tiles[g][:, first + s, :].bitcast(F32)
                 for u in range(2):
@@ -120,7 +119,7 @@ def tile_swaattention_pa_t_kernel(
             nc.scalar.mul(out=swapped[:, :, HALF:HEAD_DIM], in_=sin_tiles[g][:, :, 0:HALF], mul=-1.0)
 
         def prep_tables(g):
-            tab_ps = psum_prep.tile([P, 2, GROUP * P], BF16, name="prep")
+            tab_ps = psum_act.tile([P, 2, GROUP * P], BF16, name="evac")
             for which in range(2):
                 for s in range(GROUP):
                     nc.tensor.transpose(

@@ -204,26 +204,30 @@ def tile_swaattention_pa_t_kernel(
                 out=crossed_of[g][:, :, s, :], in0=by_head, in1=over_heads(g, 1, s), op=MULT
             )
 
-        def add_q(g, first, count):
-            a = straight_of[g][:, :, first : first + count, :]
-            b = crossed_of[g][:, :, first : first + count, :]
-            if count == GROUP:
-                halves = "p h s (e c) -> p (h s) e c"
+        def add_q(g, heads):
+            halves = "p h s (e c) -> p (h s) e c"
+            for h in range(0, HEADS, heads):
+                a = straight_of[g][:, h : h + heads, :, :]
+                b = crossed_of[g][:, h : h + heads, :, :]
                 a_halves = a.rearrange(halves, e=2)
                 b_halves = b.rearrange(halves, e=2)
                 nc.gpsimd.tensor_tensor(
                     out=a_halves, in0=a_halves, in1=b_halves[:, :, ::-1, :], op=ADD
                 )
-            else:
-                low, high = slice(0, HALF), slice(HALF, HEAD_DIM)
-                nc.gpsimd.tensor_tensor(
-                    out=a[:, :, :, low], in0=a[:, :, :, low], in1=b[:, :, :, high], op=ADD
+                nc.sync.dma_start(
+                    out=out_rows[Q][:, h : h + heads, g * GROUP : (g + 1) * GROUP, :], in_=a
                 )
-                nc.gpsimd.tensor_tensor(
-                    out=a[:, :, :, high], in0=a[:, :, :, high], in1=b[:, :, :, low], op=ADD
-                )
+
+        def add_q_slot(engine, g, s):
+            halves = "p h (e c) -> p h e c"
+            a = straight_of[g][:, :, s, :].rearrange(halves, e=2)
+            b = crossed_of[g][:, :, s, :].rearrange(halves, e=2)
+            engine.tensor_tensor(out=a, in0=a, in1=b[:, :, ::-1, :], op=ADD)
+
+        def store_q(g, first, count):
             nc.sync.dma_start(
-                out=out_rows[Q][:, :, g * GROUP + first : g * GROUP + first + count, :], in_=a
+                out=out_rows[Q][:, :, g * GROUP + first : g * GROUP + first + count, :],
+                in_=straight_of[g][:, :, first : first + count, :],
             )
 
         def mult_k(g, h):
@@ -273,6 +277,17 @@ def tile_swaattention_pa_t_kernel(
                 out=out_rows[VALUE][:, :, g * GROUP : (g + 1) * GROUP, :], in_=v_rows_of[g][:]
             )
 
+        v_done = []
+
+        def next_v(count):
+            for i in range(count):
+                slot = len(v_done)
+                if slot < SLOTS:
+                    mx_v(slot // GROUP, slot % GROUP)
+                    v_done.append(slot)
+                    if slot % GROUP == GROUP - 1:
+                        store_v(slot // GROUP)
+
         load_x(0)
         load_x(1)
         load_weight()
@@ -296,64 +311,77 @@ def tile_swaattention_pa_t_kernel(
         swap_sin(1)
         prep_tables(0)
 
-        for g in range(N_GROUPS):
-            has_next = g + 1 < N_GROUPS
-            last = not has_next
+        final = N_GROUPS - 1
+        for g in range(final):
+            next_is_final = g + 1 == final
             mult_q_gpsimd(g)
             mult_q_straight(g, 0)
             mult_q_crossed(g, 0)
             mult_q_straight(g, 1)
             mult_q_crossed(g, 1)
-            if last:
-                add_q(g, 0, 2)
             mult_q_straight(g, 2)
-            if has_next:
-                prep_tables(g + 1)
+            prep_tables(g + 1)
             if g > 0:
                 back_k(g - 1, 2)
                 back_k(g - 1, 3)
-                store_k(g - 1, 0, HEADS)
-            if g + 2 < N_GROUPS:
+                store_k(g - 1, 2, 2)
+            if not next_is_final:
                 swap_sin(g + 2)
-            if has_next:
-                quantise(g + 1)
+            quantise(g + 1)
             mult_q_crossed(g, 2)
-            if last:
-                add_q(g, 2, 2)
-            else:
-                add_q(g, 0, GROUP)
+            add_q(g, 2 if next_is_final else HEADS)
             mx_k(g, 1)
             mx_k(g, 2)
             mx_k(g, 3)
-            if has_next:
-                mx_q_copy(g + 1)
-            mx_v(g, 0)
-            mx_v(g, 1)
-            if last:
-                mx_v(g, 2)
-                mx_v(g, 3)
-                store_v(g)
+            mx_q_copy(g + 1)
+            next_v(2 + GROUP if next_is_final else 2)
             mult_k(g, 0)
-            if has_next:
+            if next_is_final:
+                mx_k(final, 0)
+            else:
                 mx_q(g + 1, 0)
             mult_k(g, 1)
-            if g + 2 < N_GROUPS:
+            if not next_is_final:
                 prep_x(g + 2, 0)
                 prep_x(g + 2, 1)
             back_k(g, 0)
             back_k(g, 1)
-            if last:
-                store_k(g, 0, 2)
+            store_k(g, 0, 2)
             mult_k(g, 2)
-            if last:
-                back_k(g, 2)
             mult_k(g, 3)
-            if has_next:
+            if next_is_final:
+                mx_k(final, 1)
+                mx_k(final, 2)
+                mx_k(final, 3)
+            else:
                 mx_q(g + 1, 1)
                 mx_q(g + 1, 2)
                 mx_k(g + 1, 0)
-                mx_v(g, 2)
-                mx_v(g, 3)
-                store_v(g)
-        back_k(N_GROUPS - 1, 3)
-        store_k(N_GROUPS - 1, 2, 2)
+            next_v(2)
+
+        mult_q_gpsimd(final)
+        add_q_slot(nc.gpsimd, final, GROUP - 1)
+        mult_k(final, 0)
+        mx_q(final, 0)
+        back_k(final - 1, 2)
+        back_k(final - 1, 3)
+        store_k(final - 1, 2, 2)
+        mult_k(final, 1)
+        mx_q(final, 1)
+        back_k(final, 0)
+        mult_k(final, 2)
+        mx_q(final, 2)
+        back_k(final, 1)
+        store_k(final, 0, 2)
+        mult_k(final, 3)
+        back_k(final, 2)
+        back_k(final, 3)
+        store_k(final, 2, 2)
+        for s in range(GROUP - 1):
+            mult_q_straight(final, s)
+            mult_q_crossed(final, s)
+            if s < GROUP - 2:
+                add_q_slot(nc.gpsimd, final, s)
+        store_q(final, 0, 2)
+        add_q_slot(nc.vector, final, GROUP - 2)
+        store_q(final, 2, 2)

@@ -129,11 +129,18 @@ def tile_swaattention_pa_t_kernel(
             nc.scalar.copy(out=table[:], in_=tab_ps[:])
             table_of[g] = table
 
-        def quantise(g):
-            codes = operands.tile([P, GROUP * P], U32, align_bytes=64)
-            scales = operands.tile([P, GROUP * P], U8, align_bytes=64)
-            nc.vector.quantize_mx(out=codes[:].bitcast(FP8X4), scales=scales[:], in_=grouped_of[g][:])
-            operand_of[g] = (codes, scales)
+        def quantise(g, first, count):
+            if first == 0:
+                codes = operands.tile([P, GROUP * P], U32, align_bytes=64)
+                scales = operands.tile([P, GROUP * P], U8, align_bytes=64)
+                operand_of[g] = (codes, scales)
+            codes, scales = operand_of[g]
+            tokens = slice(first * P, (first + count) * P)
+            nc.vector.quantize_mx(
+                out=codes[:, tokens].bitcast(FP8X4),
+                scales=scales[:, tokens],
+                in_=grouped_of[g][:, first * P * PACK : (first + count) * P * PACK],
+            )
 
         def project(bank, g, s, third):
             codes, scales = operand_of[g]
@@ -298,8 +305,9 @@ def tile_swaattention_pa_t_kernel(
             load_tables(g)
 
         prep_x(0, 0)
+        quantise(0, 0, 2)
         prep_x(0, 1)
-        quantise(0)
+        quantise(0, 2, 2)
         swap_sin(0)
         prep_x(1, 0)
         prep_x(1, 1)
@@ -327,7 +335,7 @@ def tile_swaattention_pa_t_kernel(
                 store_k(g - 1, 2, 2)
             if not next_is_final:
                 swap_sin(g + 2)
-            quantise(g + 1)
+            quantise(g + 1, 0, GROUP)
             mult_q_crossed(g, 2)
             add_q(g, 2 if next_is_final else HEADS)
             mx_k(g, 1)
@@ -361,6 +369,7 @@ def tile_swaattention_pa_t_kernel(
 
         mult_q_gpsimd(final)
         add_q_slot(nc.gpsimd, final, GROUP - 1)
+        store_q(final, GROUP - 1, 1)
         mult_k(final, 0)
         mx_q(final, 0)
         back_k(final - 1, 2)
@@ -384,4 +393,4 @@ def tile_swaattention_pa_t_kernel(
                 add_q_slot(nc.gpsimd, final, s)
         store_q(final, 0, 2)
         add_q_slot(nc.vector, final, GROUP - 2)
-        store_q(final, 2, 2)
+        store_q(final, GROUP - 2, 1)

@@ -205,10 +205,11 @@ def tile_swaattention_pa_t_kernel(
                 out=straight_of[g][:, :, s, :], in0=by_head, in1=over_heads(g, 0, s), op=MULT
             )
 
-        def mult_q_crossed(g, s):
+        def mult_q_crossed(g, s, first=0, stop=HEADS):
             by_head = bank_of[(Q, g, s)][:].rearrange("p (h d) -> p h d", h=HEADS)
+            factor = factor_tiles[g][:, 1, s, :].unsqueeze(1).to_broadcast([P, stop - first, HEAD_DIM])
             nc.vector.tensor_tensor(
-                out=crossed_of[g][:, :, s, :], in0=by_head, in1=over_heads(g, 1, s), op=MULT
+                out=crossed_of[g][:, first:stop, s, :], in0=by_head[:, first:stop, :], in1=factor, op=MULT
             )
 
         def add_q(g, heads):
@@ -328,6 +329,7 @@ def tile_swaattention_pa_t_kernel(
             mult_q_straight(g, 1)
             mult_q_crossed(g, 1)
             mult_q_straight(g, 2)
+            mult_q_crossed(g, 2, 1, HEADS)
             prep_tables(g + 1)
             if g > 0:
                 back_k(g - 1, 2)
@@ -336,7 +338,7 @@ def tile_swaattention_pa_t_kernel(
             if not next_is_final:
                 swap_sin(g + 2)
             quantise(g + 1, 0, GROUP)
-            mult_q_crossed(g, 2)
+            mult_q_crossed(g, 2, 0, 1)
             add_q(g, 2 if next_is_final else HEADS)
             mx_k(g, 1)
             mx_k(g, 2)

@@ -55,6 +55,10 @@ def tile_swaattention_pa_t_kernel(
         psum_act = stack.enter_context(tc.psum_pool(name="psum_act", bufs=4))
         stack.enter_context(tc.manual_schedule())
 
+        w_words = consts.tile([P, 2 * 3 * THIRD], U8, align_bytes=64)
+        w_scales = consts.tile([P, 3 * THIRD], U8, align_bytes=64)
+        nc.vector.memset(w_scales[:].bitcast(I32), 0)
+
         ident = consts.tile([P, P], F32)
         make_identity(nc, ident[:])
         ident_bf = consts.tile([P, P], BF16)
@@ -63,19 +67,19 @@ def tile_swaattention_pa_t_kernel(
         nc.vector.tensor_copy(out=perm[:, 0:HALF], in_=ident[:, HALF:P])
         nc.vector.tensor_copy(out=perm[:, HALF:P], in_=ident[:, 0:HALF])
 
-        w_words = consts.tile([P, 2 * 3 * THIRD], U8, align_bytes=64)
-        w_scales = consts.tile([P, 3 * THIRD], U8, align_bytes=64)
-        nc.vector.memset(w_scales[:].bitcast(I32), 0)
-
         x_tiles, factor_tiles, sin_tiles = [], [], []
         grouped_of, operand_of, table_of = {}, {}, {}
         bank_of, product_of, straight_of, crossed_of, k_rows_of, v_rows_of = {}, {}, {}, {}, {}, {}
         copy_of = {}
 
-        def load_x(g):
-            slots = slice(g * GROUP, (g + 1) * GROUP)
+        def load_x(g, pieces):
             x_g = inputs.tile([P, GROUP, K], BF16)
-            nc.sync.dma_start(out=x_g[:], in_=x_rows[:, slots, :])
+            count = GROUP // pieces
+            for first in range(0, GROUP, count):
+                nc.sync.dma_start(
+                    out=x_g[:, first : first + count, :],
+                    in_=x_rows[:, g * GROUP + first : g * GROUP + first + count, :],
+                )
             x_tiles.append(x_g)
 
         def load_tables(g):
@@ -296,13 +300,13 @@ def tile_swaattention_pa_t_kernel(
                     if slot % GROUP == GROUP - 1:
                         store_v(slot // GROUP)
 
-        load_x(0)
-        load_x(1)
+        load_x(0, 2)
         load_weight()
         load_tables(0)
+        load_x(1, 1)
         load_tables(1)
         for g in range(2, N_GROUPS):
-            load_x(g)
+            load_x(g, 1)
             load_tables(g)
 
         prep_x(0, 0)
@@ -310,11 +314,11 @@ def tile_swaattention_pa_t_kernel(
         prep_x(0, 1)
         quantise(0, 2, 2)
         swap_sin(0)
-        prep_x(1, 0)
-        prep_x(1, 1)
         mx_q(0, 0)
         mx_q(0, 1)
         mx_q(0, 2)
+        prep_x(1, 0)
+        prep_x(1, 1)
         mx_k(0, 0)
         mx_q_copy(0)
         swap_sin(1)

@@ -24,6 +24,8 @@ THIRD = HEADS * HEAD_DIM
 SLOTS = TOKENS // P
 GROUP = 4
 N_GROUPS = SLOTS // GROUP
+LOAD_SPANS = ((0, 1), (1, 1), (2, 2), (4, 4))
+V_SPANS = ((0, 1), (1, 2), (3, 2), (5, 2), (7, 1))
 WORDS = K // 2
 Q = 0
 KEY = 1
@@ -43,11 +45,11 @@ def tile_swaattention_pa_t_kernel(
 
     with ExitStack() as stack:
         consts = stack.enter_context(tc.tile_pool(name="consts", bufs=1))
-        inputs = stack.enter_context(tc.tile_pool(name="inputs", bufs=N_GROUPS))
+        inputs = stack.enter_context(tc.tile_pool(name="inputs", bufs=1))
         operands = stack.enter_context(tc.tile_pool(name="operands", bufs=2))
         tables = stack.enter_context(tc.tile_pool(name="tables", bufs=3))
         pairs = stack.enter_context(tc.tile_pool(name="pairs", bufs=3))
-        values = stack.enter_context(tc.tile_pool(name="values", bufs=3))
+        values = stack.enter_context(tc.tile_pool(name="values", bufs=2))
         keys = stack.enter_context(tc.tile_pool(name="keys", bufs=3))
         products = stack.enter_context(tc.tile_pool(name="products", bufs=6))
         copies = stack.enter_context(tc.tile_pool(name="copies", bufs=2))
@@ -67,29 +69,32 @@ def tile_swaattention_pa_t_kernel(
         nc.vector.tensor_copy(out=perm[:, 0:HALF], in_=ident[:, HALF:P])
         nc.vector.tensor_copy(out=perm[:, HALF:P], in_=ident[:, 0:HALF])
 
-        x_tiles, factor_tiles, sin_tiles = [], [], []
+        x_of, factors_of, sin_of = {}, {}, {}
         grouped_of, operand_of, table_of = {}, {}, {}
         bank_of, product_of, straight_of, crossed_of, k_rows_of, v_rows_of = {}, {}, {}, {}, {}, {}
         copy_of = {}
 
-        def load_x(g, pieces):
-            x_g = inputs.tile([P, GROUP, K], BF16)
-            count = GROUP // pieces
-            for first in range(0, GROUP, count):
+        def load_x(g, count, pieces):
+            slots = count * GROUP
+            x_span = inputs.tile([P, slots, K], BF16, name=f"x_{g}")
+            step = slots // pieces
+            for first in range(0, slots, step):
                 nc.sync.dma_start(
-                    out=x_g[:, first : first + count, :],
-                    in_=x_rows[:, g * GROUP + first : g * GROUP + first + count, :],
+                    out=x_span[:, first : first + step, :],
+                    in_=x_rows[:, g * GROUP + first : g * GROUP + first + step, :],
                 )
-            x_tiles.append(x_g)
+            for i in range(count):
+                x_of[g + i] = x_span[:, i * GROUP : (i + 1) * GROUP, :]
 
-        def load_tables(g):
-            slots = slice(g * GROUP, (g + 1) * GROUP)
-            factors = inputs.tile([P, 2, GROUP, HEAD_DIM], BF16)
+        def load_tables(g, count):
+            slots = slice(g * GROUP, (g + count) * GROUP)
+            factors = inputs.tile([P, 2, count * GROUP, HEAD_DIM], BF16, name=f"factors_{g}")
             nc.sync.dma_start(out=factors[:, 0, :, :], in_=cos_rows[:, slots, :])
-            factor_tiles.append(factors)
-            sin_g = inputs.tile([P, GROUP, HEAD_DIM], BF16)
-            nc.sync.dma_start(out=sin_g[:], in_=sin_rows[:, slots, :])
-            sin_tiles.append(sin_g)
+            sin_span = inputs.tile([P, count * GROUP, HEAD_DIM], BF16, name=f"sin_{g}")
+            nc.sync.dma_start(out=sin_span[:], in_=sin_rows[:, slots, :])
+            for i in range(count):
+                factors_of[g + i] = factors[:, :, i * GROUP : (i + 1) * GROUP, :]
+                sin_of[g + i] = sin_span[:, i * GROUP : (i + 1) * GROUP, :]
 
         def load_weight():
             for quadrant in range(4):
@@ -109,7 +114,7 @@ def tile_swaattention_pa_t_kernel(
             first = 2 * half
             xt = psum_act.tile([P, 2, 2, P], F32, name="evac")
             for s in range(2):
-                words = x_tiles[g][:, first + s, :].bitcast(F32)
+                words = x_of[g][:, first + s, :].bitcast(F32)
                 for u in range(2):
                     nc.tensor.transpose(xt[:, s, u, :], words[:, u:WORDS:2], ident[:])
             nc.scalar.copy(
@@ -118,16 +123,16 @@ def tile_swaattention_pa_t_kernel(
             )
 
         def swap_sin(g):
-            swapped = factor_tiles[g][:, 1, :, :]
-            nc.scalar.copy(out=swapped[:, :, 0:HALF], in_=sin_tiles[g][:, :, HALF:HEAD_DIM])
-            nc.scalar.mul(out=swapped[:, :, HALF:HEAD_DIM], in_=sin_tiles[g][:, :, 0:HALF], mul=-1.0)
+            swapped = factors_of[g][:, 1, :, :]
+            nc.scalar.copy(out=swapped[:, :, 0:HALF], in_=sin_of[g][:, :, HALF:HEAD_DIM])
+            nc.scalar.mul(out=swapped[:, :, HALF:HEAD_DIM], in_=sin_of[g][:, :, 0:HALF], mul=-1.0)
 
         def prep_tables(g):
             tab_ps = psum_act.tile([P, 2, GROUP * P], BF16, name="evac")
             for which in range(2):
                 for s in range(GROUP):
                     nc.tensor.transpose(
-                        tab_ps[:, which, s * P : (s + 1) * P], factor_tiles[g][:, which, s, :], ident_bf[:]
+                        tab_ps[:, which, s * P : (s + 1) * P], factors_of[g][:, which, s, :], ident_bf[:]
                     )
             table = tables.tile([P, 2, GROUP * P], BF16)
             nc.scalar.copy(out=table[:], in_=tab_ps[:])
@@ -180,7 +185,7 @@ def tile_swaattention_pa_t_kernel(
             bank_of[(KEY, g, h)] = bank
 
         def over_heads(g, which, s):
-            return factor_tiles[g][:, which, s, :].unsqueeze(1).to_broadcast([P, HEADS, HEAD_DIM])
+            return factors_of[g][:, which, s, :].unsqueeze(1).to_broadcast([P, HEADS, HEAD_DIM])
 
         def mx_q_copy(g):
             bank = psum_act.tile([P, THIRD], F32, name="evac")
@@ -199,7 +204,7 @@ def tile_swaattention_pa_t_kernel(
             nc.gpsimd.tensor_tensor(
                 out=pair[:, :, :, s, :],
                 in0=by_head.unsqueeze(1).to_broadcast(shape),
-                in1=factor_tiles[g][:, :, s, :].unsqueeze(2).to_broadcast(shape),
+                in1=factors_of[g][:, :, s, :].unsqueeze(2).to_broadcast(shape),
                 op=MULT,
             )
 
@@ -211,7 +216,7 @@ def tile_swaattention_pa_t_kernel(
 
         def mult_q_crossed(g, s, first=0, stop=HEADS):
             by_head = bank_of[(Q, g, s)][:].rearrange("p (h d) -> p h d", h=HEADS)
-            factor = factor_tiles[g][:, 1, s, :].unsqueeze(1).to_broadcast([P, stop - first, HEAD_DIM])
+            factor = factors_of[g][:, 1, s, :].unsqueeze(1).to_broadcast([P, stop - first, HEAD_DIM])
             nc.vector.tensor_tensor(
                 out=crossed_of[g][:, first:stop, s, :], in0=by_head[:, first:stop, :], in1=factor, op=MULT
             )
@@ -274,20 +279,24 @@ def tile_swaattention_pa_t_kernel(
                 in_=k_rows_of[g][:, first : first + count, :, :],
             )
 
+        span_of = {g: (first, count) for first, count in V_SPANS for g in range(first, first + count)}
+
         def mx_v(g, s):
-            if s == 0:
-                v_rows = values.tile([P, HEADS, GROUP, HEAD_DIM], F32)
-                v_rows_of[g] = v_rows
+            first, count = span_of[g]
+            if (g, s) == (first, 0):
+                v_rows = values.tile([P, HEADS, count * GROUP, HEAD_DIM], F32)
+                v_rows_of[first] = v_rows
             bank = psum_act.tile([P, THIRD], F32, name="evac")
             project(bank, g, s, VALUE)
             nc.scalar.copy(
-                out=v_rows_of[g][:, :, s, :], in_=bank[:].rearrange("p (h d) -> p h d", h=HEADS)
+                out=v_rows_of[first][:, :, (g - first) * GROUP + s, :],
+                in_=bank[:].rearrange("p (h d) -> p h d", h=HEADS),
             )
-
-        def store_v(g):
-            nc.scalar.dma_start(
-                out=out_rows[VALUE][:, :, g * GROUP : (g + 1) * GROUP, :], in_=v_rows_of[g][:]
-            )
+            if (g, s) == (first + count - 1, GROUP - 1):
+                nc.scalar.dma_start(
+                    out=out_rows[VALUE][:, :, first * GROUP : (first + count) * GROUP, :],
+                    in_=v_rows_of[first][:],
+                )
 
         v_done = []
 
@@ -297,17 +306,12 @@ def tile_swaattention_pa_t_kernel(
                 if slot < SLOTS:
                     mx_v(slot // GROUP, slot % GROUP)
                     v_done.append(slot)
-                    if slot % GROUP == GROUP - 1:
-                        store_v(slot // GROUP)
 
-        load_x(0, 2)
-        load_weight()
-        load_tables(0)
-        load_x(1, 1)
-        load_tables(1)
-        for g in range(2, N_GROUPS):
-            load_x(g, 1)
-            load_tables(g)
+        for g, count in LOAD_SPANS:
+            load_x(g, count, 2 if g == 0 else 1)
+            if g == 0:
+                load_weight()
+            load_tables(g, count)
 
         prep_x(0, 0)
         quantise(0, 0, 2)

@@ -23,12 +23,11 @@ HALF = HEAD_DIM // 2
 THIRD = HEADS * HEAD_DIM
 SLOTS = TOKENS // P
 GROUP = 4
-N_GROUPS = SLOTS // GROUP
+PAIR = 2 * GROUP
+N_PAIRS = SLOTS // PAIR
+ROUNDS = 2 * N_PAIRS
 LOAD_SPANS = ((0, 1), (1, 1), (2, 2), (4, 4))
-V_SPANS = ((0, 1), (1, 2), (3, 2), (5, 2), (7, 1))
 WORDS = K // 2
-Q = 0
-KEY = 1
 VALUE = 2
 
 FLOPS = 2 * TOKENS * K * 3 * THIRD
@@ -47,10 +46,9 @@ def tile_swaattention_pa_t_kernel(
         consts = stack.enter_context(tc.tile_pool(name="consts", bufs=1))
         inputs = stack.enter_context(tc.tile_pool(name="inputs", bufs=1))
         operands = stack.enter_context(tc.tile_pool(name="operands", bufs=2))
-        tables = stack.enter_context(tc.tile_pool(name="tables", bufs=3))
-        pairs = stack.enter_context(tc.tile_pool(name="pairs", bufs=3))
+        tables = stack.enter_context(tc.tile_pool(name="tables", bufs=2))
+        results = stack.enter_context(tc.tile_pool(name="results", bufs=3))
         values = stack.enter_context(tc.tile_pool(name="values", bufs=2))
-        keys = stack.enter_context(tc.tile_pool(name="keys", bufs=3))
         products = stack.enter_context(tc.tile_pool(name="products", bufs=6))
         copies = stack.enter_context(tc.tile_pool(name="copies", bufs=2))
         psum_vec = stack.enter_context(tc.psum_pool(name="psum_vec", bufs=4))
@@ -69,10 +67,9 @@ def tile_swaattention_pa_t_kernel(
         nc.vector.tensor_copy(out=perm[:, 0:HALF], in_=ident[:, HALF:P])
         nc.vector.tensor_copy(out=perm[:, HALF:P], in_=ident[:, 0:HALF])
 
-        x_of, factors_of, sin_of = {}, {}, {}
+        x_of, factors_of = {}, {}
         grouped_of, operand_of, table_of = {}, {}, {}
-        bank_of, product_of, straight_of, crossed_of, k_rows_of, v_rows_of = {}, {}, {}, {}, {}, {}
-        copy_of = {}
+        bank_of, product_of, result_of, copy_of, v_rows_of = {}, {}, {}, {}, {}
 
         def load_x(g, count, pieces):
             slots = count * GROUP
@@ -90,11 +87,9 @@ def tile_swaattention_pa_t_kernel(
             slots = slice(g * GROUP, (g + count) * GROUP)
             factors = inputs.tile([P, 2, count * GROUP, HEAD_DIM], BF16, name=f"factors_{g}")
             nc.sync.dma_start(out=factors[:, 0, :, :], in_=cos_rows[:, slots, :])
-            sin_span = inputs.tile([P, count * GROUP, HEAD_DIM], BF16, name=f"sin_{g}")
-            nc.sync.dma_start(out=sin_span[:], in_=sin_rows[:, slots, :])
+            nc.sync.dma_start(out=factors[:, 1, :, :], in_=sin_rows[:, slots, :])
             for i in range(count):
                 factors_of[g + i] = factors[:, :, i * GROUP : (i + 1) * GROUP, :]
-                sin_of[g + i] = sin_span[:, i * GROUP : (i + 1) * GROUP, :]
 
         def load_weight():
             for quadrant in range(4):
@@ -104,56 +99,63 @@ def tile_swaattention_pa_t_kernel(
                 )
             nc.sync.dma_start(out=w_words[:].bitcast(I32), in_=w_attn_words[0].bitcast(I32))
 
-        def prep_x(g, half):
-            if half == 0:
-                grouped = operands.tile([P, GROUP * P * PACK], BF16, align_bytes=64)
-                grouped_of[g] = grouped
+        def prep_x(pair, quarter):
+            if quarter == 0:
+                grouped = operands.tile([P, PAIR * P * PACK], BF16, align_bytes=64)
+                grouped_of[pair] = grouped
             grouped_words = (
-                grouped_of[g][:].bitcast(F32).rearrange("p (s r u) -> p s r u", s=GROUP, u=2)
+                grouped_of[pair][:].bitcast(F32).rearrange("p (s r u) -> p s r u", s=PAIR, u=2)
             )
-            first = 2 * half
             xt = psum_act.tile([P, 2, 2, P], F32, name="evac")
             for s in range(2):
-                words = x_of[g][:, first + s, :].bitcast(F32)
+                slot = 2 * quarter + s
+                words = x_of[2 * pair + slot // GROUP][:, slot % GROUP, :].bitcast(F32)
                 for u in range(2):
                     nc.tensor.transpose(xt[:, s, u, :], words[:, u:WORDS:2], ident[:])
             nc.scalar.copy(
-                out=grouped_words[:, first : first + 2, :, :],
+                out=grouped_words[:, 2 * quarter : 2 * quarter + 2, :, :],
                 in_=xt[:].rearrange("p s u r -> p s r u"),
             )
 
-        def swap_sin(g):
-            swapped = factors_of[g][:, 1, :, :]
-            nc.scalar.copy(out=swapped[:, :, 0:HALF], in_=sin_of[g][:, :, HALF:HEAD_DIM])
-            nc.scalar.mul(out=swapped[:, :, HALF:HEAD_DIM], in_=sin_of[g][:, :, 0:HALF], mul=-1.0)
+        def sign_sin(pair):
+            first_half = factors_of[2 * pair][:, 1, :, 0:HALF]
+            nc.scalar.mul(out=first_half, in_=first_half, mul=-1.0)
 
-        def prep_tables(g):
+        def swap_sin(pair):
+            sin = factors_of[2 * pair + 1][:, 1, :, :]
+            swapped = tables.tile([P, GROUP, HEAD_DIM], BF16)
+            nc.scalar.copy(out=swapped[:, :, 0:HALF], in_=sin[:, :, HALF:HEAD_DIM])
+            nc.scalar.mul(out=swapped[:, :, HALF:HEAD_DIM], in_=sin[:, :, 0:HALF], mul=-1.0)
+            table_of[("swapped", pair)] = swapped
+
+        def prep_tables(pair):
+            cos = factors_of[2 * pair + 1][:, 0, :, :]
             tab_ps = psum_act.tile([P, 2, GROUP * P], BF16, name="evac")
-            for which in range(2):
+            for which, source in enumerate((cos, table_of[("swapped", pair)])):
                 for s in range(GROUP):
                     nc.tensor.transpose(
-                        tab_ps[:, which, s * P : (s + 1) * P], factors_of[g][:, which, s, :], ident_bf[:]
+                        tab_ps[:, which, s * P : (s + 1) * P], source[:, s, :], ident_bf[:]
                     )
             table = tables.tile([P, 2, GROUP * P], BF16)
             nc.scalar.copy(out=table[:], in_=tab_ps[:])
-            table_of[g] = table
+            table_of[pair] = table
 
-        def quantise(g, first, count):
+        def quantise(pair, first, count):
             if first == 0:
-                codes = operands.tile([P, GROUP * P], U32, align_bytes=64)
-                scales = operands.tile([P, GROUP * P], U8, align_bytes=64)
-                operand_of[g] = (codes, scales)
-            codes, scales = operand_of[g]
+                codes = operands.tile([P, PAIR * P], U32, align_bytes=64)
+                scales = operands.tile([P, PAIR * P], U8, align_bytes=64)
+                operand_of[pair] = (codes, scales)
+            codes, scales = operand_of[pair]
             tokens = slice(first * P, (first + count) * P)
             nc.vector.quantize_mx(
                 out=codes[:, tokens].bitcast(FP8X4),
                 scales=scales[:, tokens],
-                in_=grouped_of[g][:, first * P * PACK : (first + count) * P * PACK],
+                in_=grouped_of[pair][:, first * P * PACK : (first + count) * P * PACK],
             )
 
-        def project(bank, g, s, third):
-            codes, scales = operand_of[g]
-            tokens = slice(s * P, (s + 1) * P)
+        def project(bank, slot, third):
+            codes, scales = operand_of[slot // PAIR]
+            tokens = slice(slot % PAIR * P, (slot % PAIR + 1) * P)
             nc.tensor.matmul_mx(
                 out=bank[:],
                 lhsT=codes[:, tokens].bitcast(FP8X4),
@@ -164,102 +166,97 @@ def tile_swaattention_pa_t_kernel(
                 stop=True,
             )
 
-        def mx_q(g, s):
+        def mx_straight(r, s):
             bank = psum_vec.tile([P, THIRD], F32, name="bank")
-            project(bank, g, s, Q)
-            bank_of[(Q, g, s)] = bank
+            project(bank, r // 2 * PAIR + s, r % 2)
+            bank_of[("straight", r, s)] = bank
 
-        def mx_k(g, h):
-            codes, scales = operand_of[g]
-            first = KEY * THIRD + h * HEAD_DIM
+        def mx_copy(r):
+            bank = psum_act.tile([P, THIRD], F32, name="evac")
+            project(bank, r // 2 * PAIR + GROUP - 1, r % 2)
+            copy = copies.tile([P, HEADS, 2, HEAD_DIM], F32)
+            nc.scalar.copy(out=copy[:, :, 0, :], in_=bank[:].rearrange("p (h d) -> p h d", h=HEADS))
+            halves = bank[:].rearrange("p (h e c) -> p h e c", h=HEADS, e=2)
+            nc.scalar.copy(
+                out=copy[:, :, 1, :].rearrange("p h (e c) -> p h e c", e=2), in_=halves[:, :, ::-1, :]
+            )
+            copy_of[r] = copy
+
+        def mx_turned(r, h):
+            codes, scales = operand_of[r // 2]
+            tokens = slice(GROUP * P, PAIR * P)
+            first = r % 2 * THIRD + h * HEAD_DIM
             bank = psum_vec.tile([P, GROUP * P], F32, name="bank")
             nc.tensor.matmul_mx(
                 out=bank[:],
                 lhsT=w_words[:, 2 * first : 2 * (first + HEAD_DIM)].bitcast(FP4X4),
                 lhsT_scale=w_scales[:, first : first + HEAD_DIM],
-                rhs=codes[:].bitcast(FP8X4),
-                rhs_scale=scales[:],
+                rhs=codes[:, tokens].bitcast(FP8X4),
+                rhs_scale=scales[:, tokens],
                 start=True,
                 stop=True,
             )
-            bank_of[(KEY, g, h)] = bank
+            bank_of[("turned", r, h)] = bank
 
-        def over_heads(g, which, s):
-            return factors_of[g][:, which, s, :].unsqueeze(1).to_broadcast([P, HEADS, HEAD_DIM])
-
-        def mx_q_copy(g):
-            bank = psum_act.tile([P, THIRD], F32, name="evac")
-            project(bank, g, GROUP - 1, Q)
-            q_copy = copies.tile([P, THIRD], F32)
-            nc.scalar.copy(out=q_copy[:], in_=bank[:])
-            copy_of[g] = q_copy
-
-        def mult_q_gpsimd(g):
-            pair = pairs.tile([P, 2, HEADS, GROUP, HEAD_DIM], F32)
-            straight_of[g] = pair[:, 0, :, :, :]
-            crossed_of[g] = pair[:, 1, :, :, :]
+        def mult_gpsimd(r):
+            result = results.tile([P, HEADS, PAIR + GROUP, HEAD_DIM], F32)
+            result_of[r] = result
             s = GROUP - 1
-            shape = [P, 2, HEADS, HEAD_DIM]
-            by_head = copy_of[g][:].rearrange("p (h d) -> p h d", h=HEADS)
+            factors = factors_of[r - r % 2][:, :, s, :].unsqueeze(1)
             nc.gpsimd.tensor_tensor(
-                out=pair[:, :, :, s, :],
-                in0=by_head.unsqueeze(1).to_broadcast(shape),
-                in1=factors_of[g][:, :, s, :].unsqueeze(2).to_broadcast(shape),
+                out=result[:, :, s::PAIR, :],
+                in0=copy_of[r][:],
+                in1=factors.to_broadcast([P, HEADS, 2, HEAD_DIM]),
                 op=MULT,
             )
 
-        def mult_q_straight(g, s):
-            by_head = bank_of[(Q, g, s)][:].rearrange("p (h d) -> p h d", h=HEADS)
+        def mult_plain(r, s):
+            factor = factors_of[r - r % 2][:, 0, s, :].unsqueeze(1)
             nc.vector.tensor_tensor(
-                out=straight_of[g][:, :, s, :], in0=by_head, in1=over_heads(g, 0, s), op=MULT
+                out=result_of[r][:, :, s, :],
+                in0=bank_of[("straight", r, s)][:].rearrange("p (h d) -> p h d", h=HEADS),
+                in1=factor.to_broadcast([P, HEADS, HEAD_DIM]),
+                op=MULT,
             )
 
-        def mult_q_crossed(g, s, first=0, stop=HEADS):
-            by_head = bank_of[(Q, g, s)][:].rearrange("p (h d) -> p h d", h=HEADS)
-            factor = factors_of[g][:, 1, s, :].unsqueeze(1).to_broadcast([P, stop - first, HEAD_DIM])
+        def mult_crossed(r, s, first=0, stop=HEADS):
+            halves = bank_of[("straight", r, s)][:].rearrange("p (h e c) -> p h e c", h=HEADS, e=2)
+            factor = factors_of[r - r % 2][:, 1, s, :].rearrange("p (e c) -> p e c", e=2).unsqueeze(1)
             nc.vector.tensor_tensor(
-                out=crossed_of[g][:, first:stop, s, :], in0=by_head[:, first:stop, :], in1=factor, op=MULT
+                out=result_of[r][:, first:stop, PAIR + s, :].rearrange("p h (e c) -> p h e c", e=2),
+                in0=halves[:, first:stop, ::-1, :],
+                in1=factor.to_broadcast([P, stop - first, 2, HALF]),
+                op=MULT,
             )
 
-        def add_q(g, heads):
-            halves = "p h s (e c) -> p (h s) e c"
+        def add_straight(r, heads):
             for h in range(0, HEADS, heads):
-                a = straight_of[g][:, h : h + heads, :, :]
-                b = crossed_of[g][:, h : h + heads, :, :]
-                a_halves = a.rearrange(halves, e=2)
-                b_halves = b.rearrange(halves, e=2)
-                nc.gpsimd.tensor_tensor(
-                    out=a_halves, in0=a_halves, in1=b_halves[:, :, ::-1, :], op=ADD
-                )
-                nc.sync.dma_start(
-                    out=out_rows[Q][:, h : h + heads, g * GROUP : (g + 1) * GROUP, :], in_=a
-                )
+                sums = result_of[r][:, h : h + heads, 0:GROUP, :]
+                crossed = result_of[r][:, h : h + heads, PAIR : PAIR + GROUP, :]
+                nc.gpsimd.tensor_tensor(out=sums, in0=sums, in1=crossed, op=ADD)
 
-        def add_q_slot(engine, g, s):
-            halves = "p h (e c) -> p h e c"
-            a = straight_of[g][:, :, s, :].rearrange(halves, e=2)
-            b = crossed_of[g][:, :, s, :].rearrange(halves, e=2)
-            engine.tensor_tensor(out=a, in0=a, in1=b[:, :, ::-1, :], op=ADD)
+        def add_slot(engine, r, s):
+            sums = result_of[r][:, :, s, :]
+            engine.tensor_tensor(out=sums, in0=sums, in1=result_of[r][:, :, PAIR + s, :], op=ADD)
 
-        def store_q(g, first, count):
+        def store(r, heads, slots):
+            first = r // 2 * PAIR
             nc.sync.dma_start(
-                out=out_rows[Q][:, :, g * GROUP + first : g * GROUP + first + count, :],
-                in_=straight_of[g][:, :, first : first + count, :],
+                out=out_rows[r % 2][:, heads[0] : heads[1], first + slots[0] : first + slots[1], :],
+                in_=result_of[r][:, heads[0] : heads[1], slots[0] : slots[1], :],
             )
 
-        def mult_k(g, h):
-            bank = bank_of[(KEY, g, h)]
+        def mult_turned(r, h):
+            bank = bank_of[("turned", r, h)]
+            table = table_of[r // 2]
             straight_t = products.tile([P, GROUP * P], F32)
             crossed_t = products.tile([P, GROUP * P], F32)
-            nc.vector.tensor_tensor(out=straight_t[:], in0=bank[:], in1=table_of[g][:, 0, :], op=MULT)
-            nc.vector.tensor_tensor(out=crossed_t[:], in0=bank[:], in1=table_of[g][:, 1, :], op=MULT)
-            product_of[(g, h)] = (straight_t, crossed_t)
+            nc.vector.tensor_tensor(out=straight_t[:], in0=bank[:], in1=table[:, 0, :], op=MULT)
+            nc.vector.tensor_tensor(out=crossed_t[:], in0=bank[:], in1=table[:, 1, :], op=MULT)
+            product_of[(r, h)] = (straight_t, crossed_t)
 
-        def back_k(g, h):
-            if h == 0:
-                k_rows = keys.tile([P, HEADS, GROUP, HEAD_DIM], F32)
-                k_rows_of[g] = k_rows
-            straight_t, crossed_t = product_of[(g, h)]
+        def back(r, h):
+            straight_t, crossed_t = product_of[(r, h)]
             summed = psum_act.tile([P, GROUP, HEAD_DIM], F32, name="evac")
             for s in range(GROUP):
                 tokens = slice(s * P, (s + 1) * P)
@@ -271,40 +268,33 @@ def tile_swaattention_pa_t_kernel(
                     out=summed[:, s, :], lhsT=crossed_t[:, tokens], rhs=perm[:],
                     is_transpose=True, start=False, stop=True,
                 )
-            nc.scalar.copy(out=k_rows_of[g][:, h, :, :], in_=summed[:])
-
-        def store_k(g, first, count):
-            nc.sync.dma_start(
-                out=out_rows[KEY][:, first : first + count, g * GROUP : (g + 1) * GROUP, :],
-                in_=k_rows_of[g][:, first : first + count, :, :],
-            )
-
-        span_of = {g: (first, count) for first, count in V_SPANS for g in range(first, first + count)}
-
-        def mx_v(g, s):
-            first, count = span_of[g]
-            if (g, s) == (first, 0):
-                v_rows = values.tile([P, HEADS, count * GROUP, HEAD_DIM], F32)
-                v_rows_of[first] = v_rows
-            bank = psum_act.tile([P, THIRD], F32, name="evac")
-            project(bank, g, s, VALUE)
-            nc.scalar.copy(
-                out=v_rows_of[first][:, :, (g - first) * GROUP + s, :],
-                in_=bank[:].rearrange("p (h d) -> p h d", h=HEADS),
-            )
-            if (g, s) == (first + count - 1, GROUP - 1):
-                nc.scalar.dma_start(
-                    out=out_rows[VALUE][:, :, first * GROUP : (first + count) * GROUP, :],
-                    in_=v_rows_of[first][:],
-                )
+            nc.scalar.copy(out=result_of[r][:, h, GROUP:PAIR, :], in_=summed[:])
 
         v_done = []
+        v_span_of = {
+            slot: (first, stop)
+            for first, stop in ((0,4),(4,8),(8,12),(12,16),(16,20),(20,24),(24,28),(28,32))
+            for slot in range(first, stop)
+        }
 
         def next_v(count):
             for i in range(count):
                 slot = len(v_done)
                 if slot < SLOTS:
-                    mx_v(slot // GROUP, slot % GROUP)
+                    first, stop = v_span_of[slot]
+                    if slot == first:
+                        v_rows = values.tile([P, HEADS, stop - first, HEAD_DIM], F32)
+                        v_rows_of[first] = v_rows
+                    bank = psum_act.tile([P, THIRD], F32, name="evac")
+                    project(bank, slot, VALUE)
+                    nc.scalar.copy(
+                        out=v_rows_of[first][:, :, slot - first, :],
+                        in_=bank[:].rearrange("p (h d) -> p h d", h=HEADS),
+                    )
+                    if slot == stop - 1:
+                        nc.sync.dma_start(
+                            out=out_rows[VALUE][:, :, first:stop, :], in_=v_rows_of[first][:]
+                        )
                     v_done.append(slot)
 
         for g, count in LOAD_SPANS:
@@ -317,90 +307,109 @@ def tile_swaattention_pa_t_kernel(
         quantise(0, 0, 2)
         prep_x(0, 1)
         quantise(0, 2, 2)
+        sign_sin(0)
+        mx_straight(0, 0)
+        mx_straight(0, 1)
+        mx_straight(0, 2)
+        prep_x(0, 2)
+        prep_x(0, 3)
+        mx_copy(0)
         swap_sin(0)
-        mx_q(0, 0)
-        mx_q(0, 1)
-        mx_q(0, 2)
-        prep_x(1, 0)
-        prep_x(1, 1)
-        mx_k(0, 0)
-        mx_q_copy(0)
-        swap_sin(1)
         prep_tables(0)
 
-        final = N_GROUPS - 1
-        for g in range(final):
-            next_is_final = g + 1 == final
-            mult_q_gpsimd(g)
-            mult_q_straight(g, 0)
-            mult_q_crossed(g, 0)
-            mult_q_straight(g, 1)
-            mult_q_crossed(g, 1)
-            mult_q_straight(g, 2)
-            mult_q_crossed(g, 2, 1, HEADS)
-            prep_tables(g + 1)
-            if g > 0:
-                back_k(g - 1, 2)
-                back_k(g - 1, 3)
-                store_k(g - 1, 2, 2)
-            if not next_is_final:
-                swap_sin(g + 2)
-            quantise(g + 1, 0, GROUP)
-            mult_q_crossed(g, 2, 0, 1)
-            add_q(g, 2 if next_is_final else HEADS)
-            mx_k(g, 1)
-            mx_k(g, 2)
-            mx_k(g, 3)
-            mx_q_copy(g + 1)
-            next_v(2 + GROUP if next_is_final else 2)
-            mult_k(g, 0)
-            if next_is_final:
-                mx_k(final, 0)
+        final = ROUNDS - 1
+        for r in range(final):
+            even = r % 2 == 0
+            pair = r // 2
+            more = pair + 1 < N_PAIRS
+            next_is_final = r + 1 == final
+            mult_gpsimd(r)
+            mult_plain(r, 0)
+            mult_crossed(r, 0)
+            mult_plain(r, 1)
+            mult_crossed(r, 1)
+            if r == 0:
+                quantise(0, GROUP, GROUP)
+            mult_plain(r, 2)
+            if r > 0 and more:
+                for quarter in (0, 1) if even else (2, 3):
+                    prep_x(pair + 1, quarter)
+            if r > 0:
+                back(r - 1, 2)
+                back(r - 1, 3)
+                if r == 1:
+                    store(r - 1, (2, 4), (0, PAIR))
+                else:
+                    store(r - 1, (2, 4), (0, PAIR))
+            if more:
+                if even:
+                    sign_sin(pair + 1)
+                else:
+                    swap_sin(pair + 1)
+            if more and not even:
+                mult_crossed(r, 2, 1, HEADS)
+                quantise(pair + 1, 0, PAIR)
+                mult_crossed(r, 2, 0, 1)
             else:
-                mx_q(g + 1, 0)
-            mult_k(g, 1)
-            if not next_is_final:
-                prep_x(g + 2, 0)
-                prep_x(g + 2, 1)
-            back_k(g, 0)
-            back_k(g, 1)
-            store_k(g, 0, 2)
-            mult_k(g, 2)
-            mult_k(g, 3)
+                mult_crossed(r, 2)
+            add_straight(r, 2)
+            if r == 0:
+                mx_turned(0, 0)
+            mx_turned(r, 1)
+            mx_turned(r, 2)
+            next_v([2,3,3,3,2,2,2,0][r])
+            mx_copy(r + 1)
+            mx_turned(r, 3)
+            mult_turned(r, 0)
             if next_is_final:
-                mx_k(final, 1)
-                mx_k(final, 2)
-                mx_k(final, 3)
+                mx_turned(final, 0)
             else:
-                mx_q(g + 1, 1)
-                mx_q(g + 1, 2)
-                mx_k(g + 1, 0)
-            next_v(2)
+                mx_straight(r + 1, 0)
+            mult_turned(r, 1)
+            if r == 0:
+                prep_x(1, 0)
+                prep_x(1, 1)
+            back(r, 0)
+            back(r, 1)
+            store(r, (0, 2), (0, PAIR))
+            if more and not even:
+                prep_tables(pair + 1)
+            mult_turned(r, 2)
+            mult_turned(r, 3)
+            if next_is_final:
+                mx_turned(final, 1)
+                mx_turned(final, 2)
+                mx_turned(final, 3)
+            else:
+                mx_straight(r + 1, 1)
+                mx_straight(r + 1, 2)
+                mx_turned(r + 1, 0)
+            next_v([3,2,2,2,2,2,2,0][r])
 
-        mult_q_gpsimd(final)
-        add_q_slot(nc.gpsimd, final, GROUP - 1)
-        store_q(final, GROUP - 1, 1)
-        mult_k(final, 0)
-        mx_q(final, 0)
-        back_k(final - 1, 2)
-        back_k(final - 1, 3)
-        store_k(final - 1, 2, 2)
-        mult_k(final, 1)
-        mx_q(final, 1)
-        back_k(final, 0)
-        mult_k(final, 2)
-        mx_q(final, 2)
-        back_k(final, 1)
-        store_k(final, 0, 2)
-        mult_k(final, 3)
-        back_k(final, 2)
-        back_k(final, 3)
-        store_k(final, 2, 2)
+        mult_gpsimd(final)
+        add_slot(nc.gpsimd, final, GROUP - 1)
+        mult_turned(final, 0)
+        mx_straight(final, 0)
+        back(final - 1, 2)
+        back(final - 1, 3)
+        store(final - 1, (2, 4), (0, PAIR))
+        store(final, (0, HEADS), (GROUP - 1, GROUP))
+        mult_turned(final, 1)
+        mx_straight(final, 1)
+        back(final, 0)
+        mult_turned(final, 2)
+        mx_straight(final, 2)
+        back(final, 1)
+        store(final, (0, 2), (GROUP, PAIR))
+        mult_turned(final, 3)
+        back(final, 2)
+        back(final, 3)
+        store(final, (2, 4), (GROUP, PAIR))
         for s in range(GROUP - 1):
-            mult_q_straight(final, s)
-            mult_q_crossed(final, s)
+            mult_plain(final, s)
+            mult_crossed(final, s)
             if s < GROUP - 2:
-                add_q_slot(nc.gpsimd, final, s)
-        store_q(final, 0, 2)
-        add_q_slot(nc.vector, final, GROUP - 2)
-        store_q(final, GROUP - 2, 1)
+                add_slot(nc.gpsimd, final, s)
+        store(final, (0, HEADS), (0, 2))
+        add_slot(nc.vector, final, GROUP - 2)
+        store(final, (0, HEADS), (GROUP - 2, GROUP - 1))

@@ -23,10 +23,10 @@ HALF = HEAD_DIM // 2
 THIRD = HEADS * HEAD_DIM
 SLOTS = TOKENS // P
 GROUP = 4
+N_GROUPS = SLOTS // GROUP
 PAIR = 2 * GROUP
 N_PAIRS = SLOTS // PAIR
 ROUNDS = 2 * N_PAIRS
-LOAD_SPANS = ((0, 1), (1, 1), (2, 2), (4, 4))
 WORDS = K // 2
 VALUE = 2
 
@@ -47,13 +47,24 @@ def tile_swaattention_pa_t_kernel(
         inputs = stack.enter_context(tc.tile_pool(name="inputs", bufs=1))
         operands = stack.enter_context(tc.tile_pool(name="operands", bufs=2))
         tables = stack.enter_context(tc.tile_pool(name="tables", bufs=2))
-        results = stack.enter_context(tc.tile_pool(name="results", bufs=3))
-        values = stack.enter_context(tc.tile_pool(name="values", bufs=2))
+        pairs = stack.enter_context(tc.tile_pool(name="pairs", bufs=3))
+        values = stack.enter_context(tc.tile_pool(name="values", bufs=3))
+        turned = stack.enter_context(tc.tile_pool(name="turned", bufs=3))
         products = stack.enter_context(tc.tile_pool(name="products", bufs=6))
         copies = stack.enter_context(tc.tile_pool(name="copies", bufs=2))
         psum_vec = stack.enter_context(tc.psum_pool(name="psum_vec", bufs=4))
         psum_act = stack.enter_context(tc.psum_pool(name="psum_act", bufs=4))
         stack.enter_context(tc.manual_schedule())
+
+        zeros = consts.tile([P, THIRD], BF16)
+        nc.vector.memset(zeros[:].bitcast(I32), 0)
+        idle_bank = psum_vec.tile([P, THIRD], F32, name="bank")
+
+        def spin(count):
+            for i in range(count):
+                nc.tensor.matmul(
+                    out=idle_bank[:], lhsT=zeros[:, 0:P], rhs=zeros[:], start=True, stop=True
+                )
 
         w_words = consts.tile([P, 2 * 3 * THIRD], U8, align_bytes=64)
         w_scales = consts.tile([P, 3 * THIRD], U8, align_bytes=64)
@@ -62,83 +73,81 @@ def tile_swaattention_pa_t_kernel(
         ident = consts.tile([P, P], F32)
         make_identity(nc, ident[:])
         ident_bf = consts.tile([P, P], BF16)
-        make_identity(nc, ident_bf[:])
         perm = consts.tile([P, P], F32)
-        nc.vector.tensor_copy(out=perm[:, 0:HALF], in_=ident[:, HALF:P])
-        nc.vector.tensor_copy(out=perm[:, HALF:P], in_=ident[:, 0:HALF])
 
-        x_of, factors_of = {}, {}
+        x_of, factors_of, sin_of = {}, {}, {}
         grouped_of, operand_of, table_of = {}, {}, {}
-        bank_of, product_of, result_of, copy_of, v_rows_of = {}, {}, {}, {}, {}
+        bank_of, product_of, straight_of, crossed_of, rows_of, v_rows_of = {}, {}, {}, {}, {}, {}
+        copy_of, pair_of = {}, {}
 
-        def load_x(g, count, pieces):
-            slots = count * GROUP
-            x_span = inputs.tile([P, slots, K], BF16, name=f"x_{g}")
-            step = slots // pieces
-            for first in range(0, slots, step):
-                nc.sync.dma_start(
-                    out=x_span[:, first : first + step, :],
-                    in_=x_rows[:, g * GROUP + first : g * GROUP + first + step, :],
-                )
+        def new_x(g, count):
+            x_span = inputs.tile([P, count * GROUP, K], BF16, name=f"x_{g}")
             for i in range(count):
                 x_of[g + i] = x_span[:, i * GROUP : (i + 1) * GROUP, :]
+            return x_span
 
-        def load_tables(g, count):
+        def load_x(x_span, g, first, count):
+            start = g * GROUP + first
+            nc.sync.dma_start(
+                out=x_span[:, first : first + count, :], in_=x_rows[:, start : start + count, :]
+            )
+
+        def load_tables(engine, g, count):
             slots = slice(g * GROUP, (g + count) * GROUP)
             factors = inputs.tile([P, 2, count * GROUP, HEAD_DIM], BF16, name=f"factors_{g}")
-            nc.sync.dma_start(out=factors[:, 0, :, :], in_=cos_rows[:, slots, :])
-            nc.sync.dma_start(out=factors[:, 1, :, :], in_=sin_rows[:, slots, :])
+            engine.dma_start(out=factors[:, 0, :, :], in_=cos_rows[:, slots, :])
+            sin_span = inputs.tile([P, count * GROUP, HEAD_DIM], BF16, name=f"sin_{g}")
+            engine.dma_start(out=sin_span[:], in_=sin_rows[:, slots, :])
             for i in range(count):
                 factors_of[g + i] = factors[:, :, i * GROUP : (i + 1) * GROUP, :]
+                sin_of[g + i] = sin_span[:, i * GROUP : (i + 1) * GROUP, :]
 
-        def load_weight():
+        def load_scales():
             for quadrant in range(4):
                 nc.sync.dma_start(
                     out=w_scales[32 * quadrant : 32 * quadrant + 4, :].bitcast(I32),
                     in_=w_attn_scales[0, 4 * quadrant : 4 * quadrant + 4, :].bitcast(I32),
                 )
-            nc.sync.dma_start(out=w_words[:].bitcast(I32), in_=w_attn_words[0].bitcast(I32))
 
-        def prep_x(pair, quarter):
-            if quarter == 0:
+        def load_words(third):
+            columns = slice(2 * third * THIRD, 2 * (third + 1) * THIRD)
+            nc.sync.dma_start(
+                out=w_words[:, columns].bitcast(I32), in_=w_attn_words[0][:, columns].bitcast(I32)
+            )
+
+        def prep_x(pair, first, count):
+            if first == 0:
                 grouped = operands.tile([P, PAIR * P * PACK], BF16, align_bytes=64)
                 grouped_of[pair] = grouped
             grouped_words = (
                 grouped_of[pair][:].bitcast(F32).rearrange("p (s r u) -> p s r u", s=PAIR, u=2)
             )
             xt = psum_act.tile([P, 2, 2, P], F32, name="evac")
-            for s in range(2):
-                slot = 2 * quarter + s
+            for s in range(count):
+                slot = first + s
                 words = x_of[2 * pair + slot // GROUP][:, slot % GROUP, :].bitcast(F32)
                 for u in range(2):
                     nc.tensor.transpose(xt[:, s, u, :], words[:, u:WORDS:2], ident[:])
             nc.scalar.copy(
-                out=grouped_words[:, 2 * quarter : 2 * quarter + 2, :, :],
-                in_=xt[:].rearrange("p s u r -> p s r u"),
+                out=grouped_words[:, first : first + count, :, :],
+                in_=xt[:, 0:count, :, :].rearrange("p s u r -> p s r u"),
             )
 
-        def sign_sin(pair):
-            first_half = factors_of[2 * pair][:, 1, :, 0:HALF]
-            nc.scalar.mul(out=first_half, in_=first_half, mul=-1.0)
+        def swap_sin(g):
+            swapped = factors_of[g][:, 1, :, :]
+            nc.scalar.copy(out=swapped[:, :, 0:HALF], in_=sin_of[g][:, :, HALF:HEAD_DIM])
+            nc.scalar.mul(out=swapped[:, :, HALF:HEAD_DIM], in_=sin_of[g][:, :, 0:HALF], mul=-1.0)
 
-        def swap_sin(pair):
-            sin = factors_of[2 * pair + 1][:, 1, :, :]
-            swapped = tables.tile([P, GROUP, HEAD_DIM], BF16)
-            nc.scalar.copy(out=swapped[:, :, 0:HALF], in_=sin[:, :, HALF:HEAD_DIM])
-            nc.scalar.mul(out=swapped[:, :, HALF:HEAD_DIM], in_=sin[:, :, 0:HALF], mul=-1.0)
-            table_of[("swapped", pair)] = swapped
-
-        def prep_tables(pair):
-            cos = factors_of[2 * pair + 1][:, 0, :, :]
+        def prep_tables(g):
             tab_ps = psum_act.tile([P, 2, GROUP * P], BF16, name="evac")
-            for which, source in enumerate((cos, table_of[("swapped", pair)])):
+            for which in range(2):
                 for s in range(GROUP):
                     nc.tensor.transpose(
-                        tab_ps[:, which, s * P : (s + 1) * P], source[:, s, :], ident_bf[:]
+                        tab_ps[:, which, s * P : (s + 1) * P], factors_of[g][:, which, s, :], ident_bf[:]
                     )
             table = tables.tile([P, 2, GROUP * P], BF16)
             nc.scalar.copy(out=table[:], in_=tab_ps[:])
-            table_of[pair] = table
+            table_of[g] = table
 
         def quantise(pair, first, count):
             if first == 0:
@@ -168,24 +177,20 @@ def tile_swaattention_pa_t_kernel(
 
         def mx_straight(r, s):
             bank = psum_vec.tile([P, THIRD], F32, name="bank")
-            project(bank, r // 2 * PAIR + s, r % 2)
+            project(bank, (r - r % 2) * GROUP + s, (r % 2))
             bank_of[("straight", r, s)] = bank
 
         def mx_copy(r):
             bank = psum_act.tile([P, THIRD], F32, name="evac")
-            project(bank, r // 2 * PAIR + GROUP - 1, r % 2)
-            copy = copies.tile([P, HEADS, 2, HEAD_DIM], F32)
-            nc.scalar.copy(out=copy[:, :, 0, :], in_=bank[:].rearrange("p (h d) -> p h d", h=HEADS))
-            halves = bank[:].rearrange("p (h e c) -> p h e c", h=HEADS, e=2)
-            nc.scalar.copy(
-                out=copy[:, :, 1, :].rearrange("p h (e c) -> p h e c", e=2), in_=halves[:, :, ::-1, :]
-            )
+            project(bank, (r - r % 2) * GROUP + GROUP - 1, (r % 2))
+            copy = copies.tile([P, THIRD], F32)
+            nc.scalar.copy(out=copy[:], in_=bank[:])
             copy_of[r] = copy
 
         def mx_turned(r, h):
             codes, scales = operand_of[r // 2]
             tokens = slice(GROUP * P, PAIR * P)
-            first = r % 2 * THIRD + h * HEAD_DIM
+            first = (r % 2) * THIRD + h * HEAD_DIM
             bank = psum_vec.tile([P, GROUP * P], F32, name="bank")
             nc.tensor.matmul_mx(
                 out=bank[:],
@@ -198,57 +203,60 @@ def tile_swaattention_pa_t_kernel(
             )
             bank_of[("turned", r, h)] = bank
 
+        def new_result(r):
+            pair = pairs.tile([P, 2, HEADS, GROUP, HEAD_DIM], F32)
+            pair_of[r] = pair
+            straight_of[r] = pair[:, 0, :, :, :]
+            crossed_of[r] = pair[:, 1, :, :, :]
+
         def mult_gpsimd(r):
-            result = results.tile([P, HEADS, PAIR + GROUP, HEAD_DIM], F32)
-            result_of[r] = result
+            pair = pair_of[r]
             s = GROUP - 1
-            factors = factors_of[r - r % 2][:, :, s, :].unsqueeze(1)
+            shape = [P, 2, HEADS, HEAD_DIM]
+            by_head = copy_of[r][:].rearrange("p (h d) -> p h d", h=HEADS)
             nc.gpsimd.tensor_tensor(
-                out=result[:, :, s::PAIR, :],
-                in0=copy_of[r][:],
-                in1=factors.to_broadcast([P, HEADS, 2, HEAD_DIM]),
+                out=pair[:, :, :, s, :],
+                in0=by_head.unsqueeze(1).to_broadcast(shape),
+                in1=factors_of[(r - r % 2)][:, :, s, :].unsqueeze(2).to_broadcast(shape),
                 op=MULT,
             )
 
-        def mult_plain(r, s):
-            factor = factors_of[r - r % 2][:, 0, s, :].unsqueeze(1)
+        def mult_straight(r, s, which, first=0, stop=HEADS):
+            by_head = bank_of[("straight", r, s)][:].rearrange("p (h d) -> p h d", h=HEADS)
+            factor = factors_of[(r - r % 2)][:, which, s, :].unsqueeze(1)
+            product = (straight_of, crossed_of)[which][r]
             nc.vector.tensor_tensor(
-                out=result_of[r][:, :, s, :],
-                in0=bank_of[("straight", r, s)][:].rearrange("p (h d) -> p h d", h=HEADS),
-                in1=factor.to_broadcast([P, HEADS, HEAD_DIM]),
-                op=MULT,
-            )
-
-        def mult_crossed(r, s, first=0, stop=HEADS):
-            halves = bank_of[("straight", r, s)][:].rearrange("p (h e c) -> p h e c", h=HEADS, e=2)
-            factor = factors_of[r - r % 2][:, 1, s, :].rearrange("p (e c) -> p e c", e=2).unsqueeze(1)
-            nc.vector.tensor_tensor(
-                out=result_of[r][:, first:stop, PAIR + s, :].rearrange("p h (e c) -> p h e c", e=2),
-                in0=halves[:, first:stop, ::-1, :],
-                in1=factor.to_broadcast([P, stop - first, 2, HALF]),
+                out=product[:, first:stop, s, :],
+                in0=by_head[:, first:stop, :],
+                in1=factor.to_broadcast([P, stop - first, HEAD_DIM]),
                 op=MULT,
             )
 
         def add_straight(r, heads):
+            halves = "p h s (e c) -> p (h s) e c"
             for h in range(0, HEADS, heads):
-                sums = result_of[r][:, h : h + heads, 0:GROUP, :]
-                crossed = result_of[r][:, h : h + heads, PAIR : PAIR + GROUP, :]
-                nc.gpsimd.tensor_tensor(out=sums, in0=sums, in1=crossed, op=ADD)
+                a_halves = straight_of[r][:, h : h + heads, :, :].rearrange(halves, e=2)
+                b_halves = crossed_of[r][:, h : h + heads, :, :].rearrange(halves, e=2)
+                nc.gpsimd.tensor_tensor(
+                    out=a_halves, in0=a_halves, in1=b_halves[:, :, ::-1, :], op=ADD
+                )
 
         def add_slot(engine, r, s):
-            sums = result_of[r][:, :, s, :]
-            engine.tensor_tensor(out=sums, in0=sums, in1=result_of[r][:, :, PAIR + s, :], op=ADD)
+            halves = "p h (e c) -> p h e c"
+            a = straight_of[r][:, :, s, :].rearrange(halves, e=2)
+            b = crossed_of[r][:, :, s, :].rearrange(halves, e=2)
+            engine.tensor_tensor(out=a, in0=a, in1=b[:, :, ::-1, :], op=ADD)
 
-        def store(r, heads, slots):
-            first = r // 2 * PAIR
+        def store_straight(r, heads, slots):
+            first = (r - r % 2) * GROUP
             nc.sync.dma_start(
-                out=out_rows[r % 2][:, heads[0] : heads[1], first + slots[0] : first + slots[1], :],
-                in_=result_of[r][:, heads[0] : heads[1], slots[0] : slots[1], :],
+                out=out_rows[(r % 2)][:, heads[0] : heads[1], first + slots[0] : first + slots[1], :],
+                in_=straight_of[r][:, heads[0] : heads[1], slots[0] : slots[1], :],
             )
 
         def mult_turned(r, h):
             bank = bank_of[("turned", r, h)]
-            table = table_of[r // 2]
+            table = table_of[(r - r % 2 + 1)]
             straight_t = products.tile([P, GROUP * P], F32)
             crossed_t = products.tile([P, GROUP * P], F32)
             nc.vector.tensor_tensor(out=straight_t[:], in0=bank[:], in1=table[:, 0, :], op=MULT)
@@ -256,6 +264,9 @@ def tile_swaattention_pa_t_kernel(
             product_of[(r, h)] = (straight_t, crossed_t)
 
         def back(r, h):
+            if h == 0:
+                rows = turned.tile([P, HEADS, GROUP, HEAD_DIM], F32)
+                rows_of[r] = rows
             straight_t, crossed_t = product_of[(r, h)]
             summed = psum_act.tile([P, GROUP, HEAD_DIM], F32, name="evac")
             for s in range(GROUP):
@@ -268,14 +279,30 @@ def tile_swaattention_pa_t_kernel(
                     out=summed[:, s, :], lhsT=crossed_t[:, tokens], rhs=perm[:],
                     is_transpose=True, start=False, stop=True,
                 )
-            nc.scalar.copy(out=result_of[r][:, h, GROUP:PAIR, :], in_=summed[:])
+            nc.scalar.copy(out=rows_of[r][:, h, :, :], in_=summed[:])
+
+        def store_turned(r, first, count):
+            slots = slice((r - r % 2 + 1) * GROUP, ((r - r % 2 + 1) + 1) * GROUP)
+            nc.sync.dma_start(
+                out=out_rows[(r % 2)][:, first : first + count, slots, :],
+                in_=rows_of[r][:, first : first + count, :, :],
+            )
+
+        def mult_plain(r, s):
+            mult_straight(r, s, 0)
+
+        def mult_crossed(r, s, first=0, stop=HEADS):
+            mult_straight(r, s, 1, first, stop)
+
+        def store_first(r):
+            store_turned(r, 0, 2)
+
+        def store_rest(r):
+            store_straight(r, (0, HEADS), (0, GROUP))
+            store_turned(r, 2, 2)
 
         v_done = []
-        v_span_of = {
-            slot: (first, stop)
-            for first, stop in ((0,4),(4,8),(8,12),(12,16),(16,20),(20,24),(24,28),(28,32))
-            for slot in range(first, stop)
-        }
+        v_span_of = {slot: (slot - slot % GROUP, slot - slot % GROUP + GROUP) for slot in range(SLOTS)}
 
         def next_v(count):
             for i in range(count):
@@ -297,83 +324,179 @@ def tile_swaattention_pa_t_kernel(
                         )
                     v_done.append(slot)
 
-        for g, count in LOAD_SPANS:
-            load_x(g, count, 2 if g == 0 else 1)
-            if g == 0:
-                load_weight()
-            load_tables(g, count)
 
-        prep_x(0, 0)
-        quantise(0, 0, 2)
-        prep_x(0, 1)
-        quantise(0, 2, 2)
-        sign_sin(0)
+        x_0, x_1, x_2, x_4 = new_x(0, 1), new_x(1, 1), new_x(2, 2), new_x(4, 4)
+        load_x(x_0, 0, 0, 1)
+        load_words(0)
+        load_x(x_0, 0, 1, 1)
+        load_scales()
+        load_tables(nc.sync, 0, 1)
+        load_x(x_0, 0, 2, 2)
+        load_words(1)
+        load_x(x_1, 1, 0, GROUP)
+        load_tables(nc.sync, 1, 1)
+        load_words(VALUE)
+        load_x(x_2, 2, 0, PAIR)
+        load_tables(nc.sync, 2, 2)
+        load_x(x_4, 4, 0, 2 * PAIR)
+        load_tables(nc.sync, 4, 4)
+
+        make_identity(nc, ident_bf[:])
+        nc.vector.tensor_copy(out=perm[:, 0:HALF], in_=ident[:, HALF:P])
+        nc.vector.tensor_copy(out=perm[:, HALF:P], in_=ident[:, 0:HALF])
+
+        spin(3)
+        prep_x(0, 0, 1)
+        quantise(0, 0, 1)
+        prep_x(0, 1, 1)
+        spin(1)
+        quantise(0, 1, 1)
         mx_straight(0, 0)
         mx_straight(0, 1)
-        mx_straight(0, 2)
-        prep_x(0, 2)
-        prep_x(0, 3)
-        mx_copy(0)
         swap_sin(0)
-        prep_tables(0)
+        prep_x(0, 2, 2)
+        new_result(0)
+        new_result(1)
+        mult_plain(0, 0)
+        mult_plain(0, 1)
+        mult_crossed(0, 0)
+        mult_crossed(0, 1)
+        quantise(0, 2, 2)
+        mx_straight(1, 0)
+        mx_straight(1, 1)
+        swap_sin(1)
+        prep_x(0, 4, 2)
+        prep_x(0, 6, 2)
+        mult_plain(1, 0)
+        mult_crossed(1, 0)
+        mult_plain(1, 1)
+        mult_crossed(1, 1)
+        quantise(0, GROUP, GROUP)
+        mx_straight(0, 2)
+        mx_copy(0)
+        prep_tables(1)
+        mult_gpsimd(0)
+        mult_plain(0, 2)
+        mult_crossed(0, 2)
+        add_straight(0, HEADS)
+        mx_turned(0, 0)
+        mx_turned(0, 1)
+        next_v(2)
+        mx_copy(1)
+        mx_turned(0, 2)
+        mult_gpsimd(1)
+        mult_turned(0, 0)
+        mx_turned(0, 3)
+        mult_turned(0, 1)
+        mx_turned(1, 0)
+        next_v(2)
+        back(0, 0)
+        back(0, 1)
+        store_first(0)
+        mult_turned(0, 2)
+        mx_turned(1, 1)
+        mult_turned(0, 3)
+        mx_turned(1, 2)
+        next_v(3)
+        mult_turned(1, 0)
+        mx_straight(1, 2)
+        prep_x(1, 0, 2)
+        prep_x(1, 2, 2)
+        prep_x(1, 4, 2)
+        prep_x(1, 6, 2)
+        back(0, 2)
+        back(0, 3)
+        store_rest(0)
+        swap_sin(2)
+        swap_sin(3)
+        mult_turned(1, 1)
+        mx_turned(1, 3)
+        back(1, 0)
+        mult_turned(1, 2)
+        mult_plain(1, 2)
+        mult_crossed(1, 2, 1, HEADS)
+        quantise(1, 0, PAIR)
+        mult_crossed(1, 2, 0, 1)
+        add_straight(1, HEADS)
+        next_v(1)
+        mx_straight(2, 0)
+        mx_copy(2)
+        mx_straight(2, 1)
+        next_v(1)
+        mult_turned(1, 3)
+        back(1, 1)
+        store_first(1)
+        prep_tables(3)
+        mx_straight(2, 2)
+        mx_turned(2, 0)
+        next_v(1)
+
+        quantised = {3: 2, 4: 3}
+        x_early = {2: ((2, 0), (2, 2)), 3: ((2, 4), (2, 6)), 4: ((3, 4), (3, 6))}
+        x_late = {3: ((3, 0), (3, 2))}
 
         final = ROUNDS - 1
-        for r in range(final):
+        for r in range(2, final):
             even = r % 2 == 0
             pair = r // 2
             more = pair + 1 < N_PAIRS
+            gate = r in quantised
             next_is_final = r + 1 == final
+            new_result(r)
             mult_gpsimd(r)
             mult_plain(r, 0)
             mult_crossed(r, 0)
             mult_plain(r, 1)
             mult_crossed(r, 1)
-            if r == 0:
-                quantise(0, GROUP, GROUP)
-            mult_plain(r, 2)
-            if r > 0 and more:
-                for quarter in (0, 1) if even else (2, 3):
-                    prep_x(pair + 1, quarter)
-            if r > 0:
-                back(r - 1, 2)
-                back(r - 1, 3)
-                if r == 1:
-                    store(r - 1, (2, 4), (0, PAIR))
-                else:
-                    store(r - 1, (2, 4), (0, PAIR))
+            for which, first in x_early.get(r, ()):
+                prep_x(which, first, 2)
+            mx_turned(r, 1)
+            if gate:
+                mx_straight(r, 2)
+            back(r - 1, 2)
+            back(r - 1, 3)
+            store_rest(r - 1)
             if more:
                 if even:
-                    sign_sin(pair + 1)
+                    swap_sin(2 * pair + 2)
                 else:
-                    swap_sin(pair + 1)
-            if more and not even:
+                    swap_sin(2 * pair + 3)
+            if gate:
+                mult_turned(r, 0)
+                mult_turned(r, 1)
+                mx_turned(r, 2)
+                next_v((0, 0, 2, 2, 2, 2, 2)[r])
+                mx_turned(r, 3)
+                back(r, 0)
+                mult_plain(r, 2)
                 mult_crossed(r, 2, 1, HEADS)
-                quantise(pair + 1, 0, PAIR)
+                quantise(quantised[r], 0, PAIR)
                 mult_crossed(r, 2, 0, 1)
+                add_straight(r, HEADS)
             else:
+                mult_plain(r, 2)
                 mult_crossed(r, 2)
-            add_straight(r, 2)
-            if r == 0:
-                mx_turned(0, 0)
-            mx_turned(r, 1)
-            mx_turned(r, 2)
-            next_v([2,3,3,3,2,2,2,0][r])
-            mx_copy(r + 1)
-            mx_turned(r, 3)
-            mult_turned(r, 0)
-            if next_is_final:
-                mx_turned(final, 0)
-            else:
-                mx_straight(r + 1, 0)
-            mult_turned(r, 1)
-            if r == 0:
-                prep_x(1, 0)
-                prep_x(1, 1)
-            back(r, 0)
+                add_straight(r, HEADS)
+                mx_turned(r, 2)
+                next_v((0, 0, 2, 2, 2, 2, 2)[r])
+                mx_copy(r + 1)
+                mx_turned(r, 3)
+                mult_turned(r, 0)
+                if next_is_final:
+                    mx_turned(final, 0)
+                else:
+                    mx_straight(r + 1, 0)
+                mult_turned(r, 1)
+                back(r, 0)
             back(r, 1)
-            store(r, (0, 2), (0, PAIR))
+            store_first(r)
+            for which, first in x_late.get(r, ()):
+                prep_x(which, first, 2)
+            if gate:
+                mx_straight(r + 1, 0)
+                mx_copy(r + 1)
             if more and not even:
-                prep_tables(pair + 1)
+                prep_tables(2 * pair + 3)
             mult_turned(r, 2)
             mult_turned(r, 3)
             if next_is_final:
@@ -382,34 +505,35 @@ def tile_swaattention_pa_t_kernel(
                 mx_turned(final, 3)
             else:
                 mx_straight(r + 1, 1)
-                mx_straight(r + 1, 2)
+                if r + 1 not in quantised:
+                    mx_straight(r + 1, 2)
                 mx_turned(r + 1, 0)
-            next_v([3,2,2,2,2,2,2,0][r])
+            next_v((0, 0, 2, 3, 4, 3, 2)[r])
 
+        new_result(final)
         mult_gpsimd(final)
         add_slot(nc.gpsimd, final, GROUP - 1)
-        mult_turned(final, 0)
-        mx_straight(final, 0)
         back(final - 1, 2)
         back(final - 1, 3)
-        store(final - 1, (2, 4), (0, PAIR))
-        store(final, (0, HEADS), (GROUP - 1, GROUP))
-        mult_turned(final, 1)
-        mx_straight(final, 1)
-        back(final, 0)
-        mult_turned(final, 2)
-        mx_straight(final, 2)
-        back(final, 1)
-        store(final, (0, 2), (GROUP, PAIR))
-        mult_turned(final, 3)
-        back(final, 2)
-        back(final, 3)
-        store(final, (2, 4), (GROUP, PAIR))
+        store_rest(final - 1)
+        store_straight(final, (0, HEADS), (GROUP - 1, GROUP))
+        for h in range(HEADS):
+            mult_turned(final, h)
+            if h < GROUP - 1:
+                mx_straight(final, h)
+            if h > 0:
+                back(final, h - 1)
+        back(final, HEADS - 1)
         for s in range(GROUP - 1):
             mult_plain(final, s)
             mult_crossed(final, s)
             if s < GROUP - 2:
                 add_slot(nc.gpsimd, final, s)
-        store(final, (0, HEADS), (0, 2))
         add_slot(nc.vector, final, GROUP - 2)
-        store(final, (0, HEADS), (GROUP - 2, GROUP - 1))
+        store_turned(final, 0, 1)
+        store_turned(final, 1, 1)
+        store_straight(final, (0, HEADS), (0, 1))
+        store_turned(final, 2, 1)
+        store_turned(final, 3, 1)
+        store_straight(final, (0, HEADS), (1, 2))
+        store_straight(final, (0, HEADS), (2, 3))

@@ -393,6 +393,8 @@ def tile_swaattention_pa_t_kernel(
         back(0, 0)
         back(0, 1)
         store_first(0)
+        prep_x(1, 0, 2)
+        prep_x(1, 2, 2)
         mult_turned(0, 2)
         mx_turned(1, 1)
         mult_turned(0, 3)
@@ -400,47 +402,40 @@ def tile_swaattention_pa_t_kernel(
         next_v(3)
         mult_turned(1, 0)
         mx_straight(1, 2)
-        prep_x(1, 0, 2)
-        prep_x(1, 2, 2)
+        swap_sin(2)
         prep_x(1, 4, 2)
         prep_x(1, 6, 2)
         back(0, 2)
         back(0, 3)
         store_rest(0)
-        swap_sin(2)
         swap_sin(3)
         mult_turned(1, 1)
         mx_turned(1, 3)
-        back(1, 0)
+        next_v(1)
         mult_turned(1, 2)
         mult_plain(1, 2)
         mult_crossed(1, 2, 1, HEADS)
         quantise(1, 0, PAIR)
         mult_crossed(1, 2, 0, 1)
         add_straight(1, HEADS)
-        next_v(1)
         mx_straight(2, 0)
         mx_copy(2)
-        mx_straight(2, 1)
-        next_v(1)
         mult_turned(1, 3)
+        back(1, 0)
         back(1, 1)
         store_first(1)
         prep_tables(3)
+        mx_straight(2, 1)
         mx_straight(2, 2)
         mx_turned(2, 0)
-        next_v(1)
-
-        quantised = {3: 2, 4: 3}
-        x_early = {2: ((2, 0), (2, 2)), 3: ((2, 4), (2, 6)), 4: ((3, 4), (3, 6))}
-        x_late = {3: ((3, 0), (3, 2))}
+        next_v(2)
 
         final = ROUNDS - 1
         for r in range(2, final):
             even = r % 2 == 0
             pair = r // 2
             more = pair + 1 < N_PAIRS
-            gate = r in quantised
+            gate = more and not even
             next_is_final = r + 1 == final
             new_result(r)
             mult_gpsimd(r)
@@ -448,13 +443,12 @@ def tile_swaattention_pa_t_kernel(
             mult_crossed(r, 0)
             mult_plain(r, 1)
             mult_crossed(r, 1)
-            for which, first in x_early.get(r, ()):
-                prep_x(which, first, 2)
-            mx_turned(r, 1)
-            if gate:
-                mx_straight(r, 2)
+            mult_plain(r, 2)
             back(r - 1, 2)
             back(r - 1, 3)
+            if more and even:
+                prep_x(pair + 1, 0, 2)
+                prep_x(pair + 1, 2, 2)
             store_rest(r - 1)
             if more:
                 if even:
@@ -462,39 +456,29 @@ def tile_swaattention_pa_t_kernel(
                 else:
                     swap_sin(2 * pair + 3)
             if gate:
-                mult_turned(r, 0)
-                mult_turned(r, 1)
-                mx_turned(r, 2)
-                next_v((0, 0, 2, 2, 2, 2, 2)[r])
-                mx_turned(r, 3)
-                back(r, 0)
-                mult_plain(r, 2)
                 mult_crossed(r, 2, 1, HEADS)
-                quantise(quantised[r], 0, PAIR)
+                quantise(pair + 1, 0, PAIR)
                 mult_crossed(r, 2, 0, 1)
-                add_straight(r, HEADS)
             else:
-                mult_plain(r, 2)
                 mult_crossed(r, 2)
-                add_straight(r, HEADS)
-                mx_turned(r, 2)
-                next_v((0, 0, 2, 2, 2, 2, 2)[r])
-                mx_copy(r + 1)
-                mx_turned(r, 3)
-                mult_turned(r, 0)
-                if next_is_final:
-                    mx_turned(final, 0)
-                else:
-                    mx_straight(r + 1, 0)
-                mult_turned(r, 1)
-                back(r, 0)
+            add_straight(r, HEADS)
+            mx_turned(r, 1)
+            mx_turned(r, 2)
+            next_v((0, 0, 2, 2, 2, 2, 2)[r])
+            mx_copy(r + 1)
+            mx_turned(r, 3)
+            mult_turned(r, 0)
+            if next_is_final:
+                mx_turned(final, 0)
+            else:
+                mx_straight(r + 1, 0)
+            mult_turned(r, 1)
+            back(r, 0)
             back(r, 1)
             store_first(r)
-            for which, first in x_late.get(r, ()):
-                prep_x(which, first, 2)
-            if gate:
-                mx_straight(r + 1, 0)
-                mx_copy(r + 1)
+            if more and even:
+                prep_x(pair + 1, 4, 2)
+                prep_x(pair + 1, 6, 2)
             if more and not even:
                 prep_tables(2 * pair + 3)
             mult_turned(r, 2)
@@ -505,10 +489,9 @@ def tile_swaattention_pa_t_kernel(
                 mx_turned(final, 3)
             else:
                 mx_straight(r + 1, 1)
-                if r + 1 not in quantised:
-                    mx_straight(r + 1, 2)
+                mx_straight(r + 1, 2)
                 mx_turned(r + 1, 0)
-            next_v((0, 0, 2, 3, 4, 3, 2)[r])
+            next_v((0, 0, 2, 2, 3, 3, 2)[r])
 
         new_result(final)
         mult_gpsimd(final)

@@ -319,13 +319,13 @@ def tile_swaattention_pa_t_kernel(
                         in_=bank[:].rearrange("p (h d) -> p h d", h=HEADS),
                     )
                     if slot == stop - 1:
-                        nc.sync.dma_start(
+                        nc.scalar.dma_start(
                             out=out_rows[VALUE][:, :, first:stop, :], in_=v_rows_of[first][:]
                         )
                     v_done.append(slot)
 
 
-        x_0, x_1, x_2, x_4 = new_x(0, 1), new_x(1, 1), new_x(2, 2), new_x(4, 4)
+        x_0, x_1 = new_x(0, 1), new_x(1, 1)
         load_x(x_0, 0, 0, 1)
         load_words(0)
         load_x(x_0, 0, 1, 1)
@@ -336,10 +336,9 @@ def tile_swaattention_pa_t_kernel(
         load_x(x_1, 1, 0, GROUP)
         load_tables(nc.sync, 1, 1)
         load_words(VALUE)
-        load_x(x_2, 2, 0, PAIR)
-        load_tables(nc.sync, 2, 2)
-        load_x(x_4, 4, 0, 2 * PAIR)
-        load_tables(nc.sync, 4, 4)
+        for g in range(2, 2 * N_PAIRS):
+            load_x(new_x(g, 1), g, 0, GROUP)
+            load_tables(nc.sync, g, 1)
 
         make_identity(nc, ident_bf[:])
         nc.vector.tensor_copy(out=perm[:, 0:HALF], in_=ident[:, HALF:P])

@@ -398,7 +398,7 @@ def tile_swaattention_pa_t_kernel(
         mx_turned(1, 1)
         mult_turned(0, 3)
         mx_turned(1, 2)
-        next_v(3)
+        next_v(2)
         mult_turned(1, 0)
         mx_straight(1, 2)
         swap_sin(2)
@@ -410,7 +410,7 @@ def tile_swaattention_pa_t_kernel(
         swap_sin(3)
         mult_turned(1, 1)
         mx_turned(1, 3)
-        next_v(1)
+        next_v(2)
         mult_turned(1, 2)
         mult_plain(1, 2)
         mult_crossed(1, 2, 1, HEADS)
@@ -490,7 +490,7 @@ def tile_swaattention_pa_t_kernel(
                 mx_straight(r + 1, 1)
                 mx_straight(r + 1, 2)
                 mx_turned(r + 1, 0)
-            next_v((0, 0, 2, 2, 3, 3, 2)[r])
+            next_v((0, 0, 3, 2, 3, 3, 1)[r])
 
         new_result(final)
         mult_gpsimd(final)

from contextlib import ExitStack

import concourse.mybir as mybir
from concourse.masks import make_identity

F32 = mybir.dt.float32
BF16 = mybir.dt.bfloat16
I32 = mybir.dt.int32
U32 = mybir.dt.uint32
U8 = mybir.dt.uint8
FP8X4 = mybir.dt.float8_e4m3fn_x4
FP4X4 = mybir.dt.float4_e2m1fn_x4
MULT = mybir.AluOpType.mult
ADD = mybir.AluOpType.add

P = 128
PACK = 4
TOKENS = 4096
K = P * PACK
HEADS = 4
HEAD_DIM = 128
HALF = HEAD_DIM // 2
THIRD = HEADS * HEAD_DIM
SLOTS = TOKENS // P
GROUP = 4
N_GROUPS = SLOTS // GROUP
PAIR = 2 * GROUP
N_PAIRS = SLOTS // PAIR
ROUNDS = 2 * N_PAIRS
WORDS = K // 2
VALUE = 2

FLOPS = 2 * TOKENS * K * 3 * THIRD


def tile_swaattention_pa_t_kernel(
    tc, x, freqs_cos, freqs_sin, w_attn_words, w_attn_scales, out_0, out_1, out_2
):
    nc = tc.nc
    x_rows = x[0].rearrange("(p n) k -> p n k", n=SLOTS)
    cos_rows = freqs_cos.rearrange("(p n) d -> p n d", n=SLOTS)
    sin_rows = freqs_sin.rearrange("(p n) d -> p n d", n=SLOTS)
    out_rows = [o[0].rearrange("h (p n) d -> p h n d", n=SLOTS) for o in (out_0, out_1, out_2)]

    with ExitStack() as stack:
        consts = stack.enter_context(tc.tile_pool(name="consts", bufs=1))
        inputs = stack.enter_context(tc.tile_pool(name="inputs", bufs=1))
        operands = stack.enter_context(tc.tile_pool(name="operands", bufs=2))
        tables = stack.enter_context(tc.tile_pool(name="tables", bufs=2))
        pairs = stack.enter_context(tc.tile_pool(name="pairs", bufs=3))
        values = stack.enter_context(tc.tile_pool(name="values", bufs=3))
        turned = stack.enter_context(tc.tile_pool(name="turned", bufs=3))
        products = stack.enter_context(tc.tile_pool(name="products", bufs=6))
        copies = stack.enter_context(tc.tile_pool(name="copies", bufs=2))
        psum_vec = stack.enter_context(tc.psum_pool(name="psum_vec", bufs=4))
        psum_act = stack.enter_context(tc.psum_pool(name="psum_act", bufs=4))
        stack.enter_context(tc.manual_schedule())

        zeros = consts.tile([P, THIRD], BF16)
        nc.vector.memset(zeros[:].bitcast(I32), 0)
        idle_bank = psum_vec.tile([P, THIRD], F32, name="bank")

        def spin(count):
            for i in range(count):
                nc.tensor.matmul(
                    out=idle_bank[:], lhsT=zeros[:, 0:P], rhs=zeros[:], start=True, stop=True
                )

        w_words = consts.tile([P, 2 * 3 * THIRD], U8, align_bytes=64)
        w_scales = consts.tile([P, 3 * THIRD], U8, align_bytes=64)
        nc.vector.memset(w_scales[:].bitcast(I32), 0)

        ident = consts.tile([P, P], F32)
        make_identity(nc, ident[:])
        ident_bf = consts.tile([P, P], BF16)
        perm = consts.tile([P, P], F32)

        x_of, factors_of, sin_of = {}, {}, {}
        grouped_of, operand_of, table_of = {}, {}, {}
        bank_of, product_of, straight_of, crossed_of, rows_of, v_rows_of = {}, {}, {}, {}, {}, {}
        copy_of, pair_of = {}, {}

        def new_x(g, count):
            x_span = inputs.tile([P, count * GROUP, K], BF16, name=f"x_{g}")
            for i in range(count):
                x_of[g + i] = x_span[:, i * GROUP : (i + 1) * GROUP, :]
            return x_span

        def load_x(x_span, g, first, count):
            start = g * GROUP + first
            nc.sync.dma_start(
                out=x_span[:, first : first + count, :], in_=x_rows[:, start : start + count, :]
            )

        def load_tables(engine, g, count):
            slots = slice(g * GROUP, (g + count) * GROUP)
            factors = inputs.tile([P, 2, count * GROUP, HEAD_DIM], BF16, name=f"factors_{g}")
            engine.dma_start(out=factors[:, 0, :, :], in_=cos_rows[:, slots, :])
            sin_span = inputs.tile([P, count * GROUP, HEAD_DIM], BF16, name=f"sin_{g}")
            engine.dma_start(out=sin_span[:], in_=sin_rows[:, slots, :])
            for i in range(count):
                factors_of[g + i] = factors[:, :, i * GROUP : (i + 1) * GROUP, :]
                sin_of[g + i] = sin_span[:, i * GROUP : (i + 1) * GROUP, :]

        def load_scales():
            for quadrant in range(4):
                nc.sync.dma_start(
                    out=w_scales[32 * quadrant : 32 * quadrant + 4, :].bitcast(I32),
                    in_=w_attn_scales[0, 4 * quadrant : 4 * quadrant + 4, :].bitcast(I32),
                )

        def load_words(third):
            columns = slice(2 * third * THIRD, 2 * (third + 1) * THIRD)
            nc.sync.dma_start(
                out=w_words[:, columns].bitcast(I32), in_=w_attn_words[0][:, columns].bitcast(I32)
            )

        def prep_x(pair, first, count):
            if first == 0:
                grouped = operands.tile([P, PAIR * P * PACK], BF16, align_bytes=64)
                grouped_of[pair] = grouped
            grouped_words = (
                grouped_of[pair][:].bitcast(F32).rearrange("p (s r u) -> p s r u", s=PAIR, u=2)
            )
            xt = psum_act.tile([P, 2, 2, P], F32, name="evac")
            for s in range(count):
                slot = first + s
                words = x_of[2 * pair + slot // GROUP][:, slot % GROUP, :].bitcast(F32)
                for u in range(2):
                    nc.tensor.transpose(xt[:, s, u, :], words[:, u:WORDS:2], ident[:])
            nc.scalar.copy(
                out=grouped_words[:, first : first + count, :, :],
                in_=xt[:, 0:count, :, :].rearrange("p s u r -> p s r u"),
            )

        def swap_sin(g):
            swapped = factors_of[g][:, 1, :, :]
            nc.scalar.copy(out=swapped[:, :, 0:HALF], in_=sin_of[g][:, :, HALF:HEAD_DIM])
            nc.scalar.mul(out=swapped[:, :, HALF:HEAD_DIM], in_=sin_of[g][:, :, 0:HALF], mul=-1.0)

        def prep_tables(g):
            tab_ps = psum_act.tile([P, 2, GROUP * P], BF16, name="evac")
            for which in range(2):
                for s in range(GROUP):
                    nc.tensor.transpose(
                        tab_ps[:, which, s * P : (s + 1) * P], factors_of[g][:, which, s, :], ident_bf[:]
                    )
            table = tables.tile([P, 2, GROUP * P], BF16)
            nc.scalar.copy(out=table[:], in_=tab_ps[:])
            table_of[g] = table

        def quantise(pair, first, count):
            if first == 0:
                codes = operands.tile([P, PAIR * P], U32, align_bytes=64)
                scales = operands.tile([P, PAIR * P], U8, align_bytes=64)
                operand_of[pair] = (codes, scales)
            codes, scales = operand_of[pair]
            tokens = slice(first * P, (first + count) * P)
            nc.vector.quantize_mx(
                out=codes[:, tokens].bitcast(FP8X4),
                scales=scales[:, tokens],
                in_=grouped_of[pair][:, first * P * PACK : (first + count) * P * PACK],
            )

        def project(bank, slot, third):
            codes, scales = operand_of[slot // PAIR]
            tokens = slice(slot % PAIR * P, (slot % PAIR + 1) * P)
            nc.tensor.matmul_mx(
                out=bank[:],
                lhsT=codes[:, tokens].bitcast(FP8X4),
                lhsT_scale=scales[:, tokens],
                rhs=w_words[:, 2 * third * THIRD : 2 * (third + 1) * THIRD].bitcast(FP4X4),
                rhs_scale=w_scales[:, third * THIRD : (third + 1) * THIRD],
                start=True,
                stop=True,
            )

        def mx_straight(r, s):
            bank = psum_vec.tile([P, THIRD], F32, name="bank")
            project(bank, (r - r % 2) * GROUP + s, (r % 2))
            bank_of[("straight", r, s)] = bank

        def mx_copy(r):
            bank = psum_act.tile([P, THIRD], F32, name="evac")
            project(bank, (r - r % 2) * GROUP + GROUP - 1, (r % 2))
            copy = copies.tile([P, THIRD], F32)
            nc.scalar.copy(out=copy[:], in_=bank[:])
            copy_of[r] = copy

        def mx_turned(r, h):
            codes, scales = operand_of[r // 2]
            tokens = slice(GROUP * P, PAIR * P)
            first = (r % 2) * THIRD + h * HEAD_DIM
            bank = psum_vec.tile([P, GROUP * P], F32, name="bank")
            nc.tensor.matmul_mx(
                out=bank[:],
                lhsT=w_words[:, 2 * first : 2 * (first + HEAD_DIM)].bitcast(FP4X4),
                lhsT_scale=w_scales[:, first : first + HEAD_DIM],
                rhs=codes[:, tokens].bitcast(FP8X4),
                rhs_scale=scales[:, tokens],
                start=True,
                stop=True,
            )
            bank_of[("turned", r, h)] = bank

        def new_result(r):
            pair = pairs.tile([P, 2, HEADS, GROUP, HEAD_DIM], F32)
            pair_of[r] = pair
            straight_of[r] = pair[:, 0, :, :, :]
            crossed_of[r] = pair[:, 1, :, :, :]

        def mult_gpsimd(r):
            pair = pair_of[r]
            s = GROUP - 1
            shape = [P, 2, HEADS, HEAD_DIM]
            by_head = copy_of[r][:].rearrange("p (h d) -> p h d", h=HEADS)
            nc.gpsimd.tensor_tensor(
                out=pair[:, :, :, s, :],
                in0=by_head.unsqueeze(1).to_broadcast(shape),
                in1=factors_of[(r - r % 2)][:, :, s, :].unsqueeze(2).to_broadcast(shape),
                op=MULT,
            )

        def mult_straight(r, s, which, first=0, stop=HEADS):
            by_head = bank_of[("straight", r, s)][:].rearrange("p (h d) -> p h d", h=HEADS)
            factor = factors_of[(r - r % 2)][:, which, s, :].unsqueeze(1)
            product = (straight_of, crossed_of)[which][r]
            nc.vector.tensor_tensor(
                out=product[:, first:stop, s, :],
                in0=by_head[:, first:stop, :],
                in1=factor.to_broadcast([P, stop - first, HEAD_DIM]),
                op=MULT,
            )

        def add_straight(r, heads):
            halves = "p h s (e c) -> p (h s) e c"
            for h in range(0, HEADS, heads):
                a_halves = straight_of[r][:, h : h + heads, :, :].rearrange(halves, e=2)
                b_halves = crossed_of[r][:, h : h + heads, :, :].rearrange(halves, e=2)
                nc.gpsimd.tensor_tensor(
                    out=a_halves, in0=a_halves, in1=b_halves[:, :, ::-1, :], op=ADD
                )

        def add_slot(engine, r, s):
            halves = "p h (e c) -> p h e c"
            a = straight_of[r][:, :, s, :].rearrange(halves, e=2)
            b = crossed_of[r][:, :, s, :].rearrange(halves, e=2)
            engine.tensor_tensor(out=a, in0=a, in1=b[:, :, ::-1, :], op=ADD)

        def store_straight(r, heads, slots):
            first = (r - r % 2) * GROUP
            nc.sync.dma_start(
                out=out_rows[(r % 2)][:, heads[0] : heads[1], first + slots[0] : first + slots[1], :],
                in_=straight_of[r][:, heads[0] : heads[1], slots[0] : slots[1], :],
            )

        def mult_turned(r, h):
            bank = bank_of[("turned", r, h)]
            table = table_of[(r - r % 2 + 1)]
            straight_t = products.tile([P, GROUP * P], F32)
            crossed_t = products.tile([P, GROUP * P], F32)
            nc.vector.tensor_tensor(out=straight_t[:], in0=bank[:], in1=table[:, 0, :], op=MULT)
            nc.vector.tensor_tensor(out=crossed_t[:], in0=bank[:], in1=table[:, 1, :], op=MULT)
            product_of[(r, h)] = (straight_t, crossed_t)

        def back(r, h):
            if h == 0:
                rows = turned.tile([P, HEADS, GROUP, HEAD_DIM], F32)
                rows_of[r] = rows
            straight_t, crossed_t = product_of[(r, h)]
            summed = psum_act.tile([P, GROUP, HEAD_DIM], F32, name="evac")
            for s in range(GROUP):
                tokens = slice(s * P, (s + 1) * P)
                nc.tensor.matmul(
                    out=summed[:, s, :], lhsT=straight_t[:, tokens], rhs=ident[:],
                    is_transpose=True, start=True, stop=False,
                )
                nc.tensor.matmul(
                    out=summed[:, s, :], lhsT=crossed_t[:, tokens], rhs=perm[:],
                    is_transpose=True, start=False, stop=True,
                )
            nc.scalar.copy(out=rows_of[r][:, h, :, :], in_=summed[:])

        def store_turned(r, first, count):
            slots = slice((r - r % 2 + 1) * GROUP, ((r - r % 2 + 1) + 1) * GROUP)
            nc.sync.dma_start(
                out=out_rows[(r % 2)][:, first : first + count, slots, :],
                in_=rows_of[r][:, first : first + count, :, :],
            )

        def mult_plain(r, s):
            mult_straight(r, s, 0)

        def mult_crossed(r, s, first=0, stop=HEADS):
            mult_straight(r, s, 1, first, stop)

        def store_first(r):
            store_turned(r, 0, 2)

        def store_rest(r):
            store_straight(r, (0, HEADS), (0, GROUP))
            store_turned(r, 2, 2)

        v_done = []
        v_span_of = {slot: (slot - slot % GROUP, slot - slot % GROUP + GROUP) for slot in range(SLOTS)}

        def next_v(count):
            for i in range(count):
                slot = len(v_done)
                if slot < SLOTS:
                    first, stop = v_span_of[slot]
                    if slot == first:
                        v_rows = values.tile([P, HEADS, stop - first, HEAD_DIM], F32)
                        v_rows_of[first] = v_rows
                    bank = psum_act.tile([P, THIRD], F32, name="evac")
                    project(bank, slot, VALUE)
                    nc.scalar.copy(
                        out=v_rows_of[first][:, :, slot - first, :],
                        in_=bank[:].rearrange("p (h d) -> p h d", h=HEADS),
                    )
                    if slot == stop - 1:
                        nc.scalar.dma_start(
                            out=out_rows[VALUE][:, :, first:stop, :], in_=v_rows_of[first][:]
                        )
                    v_done.append(slot)


        x_0, x_1 = new_x(0, 1), new_x(1, 1)
        load_x(x_0, 0, 0, 1)
        load_words(0)
        load_x(x_0, 0, 1, 1)
        load_scales()
        load_tables(nc.sync, 0, 1)
        load_x(x_0, 0, 2, 2)
        load_words(1)
        load_x(x_1, 1, 0, GROUP)
        load_tables(nc.sync, 1, 1)
        load_words(VALUE)
        for g in range(2, 2 * N_PAIRS):
            load_x(new_x(g, 1), g, 0, GROUP)
            load_tables(nc.sync, g, 1)

        make_identity(nc, ident_bf[:])
        nc.vector.tensor_copy(out=perm[:, 0:HALF], in_=ident[:, HALF:P])
        nc.vector.tensor_copy(out=perm[:, HALF:P], in_=ident[:, 0:HALF])

        spin(3)
        prep_x(0, 0, 1)
        quantise(0, 0, 1)
        prep_x(0, 1, 1)
        spin(1)
        quantise(0, 1, 1)
        mx_straight(0, 0)
        mx_straight(0, 1)
        swap_sin(0)
        prep_x(0, 2, 2)
        new_result(0)
        new_result(1)
        mult_plain(0, 0)
        mult_plain(0, 1)
        mult_crossed(0, 0)
        mult_crossed(0, 1)
        quantise(0, 2, 2)
        mx_straight(1, 0)
        mx_straight(1, 1)
        swap_sin(1)
        prep_x(0, 4, 2)
        prep_x(0, 6, 2)
        mult_plain(1, 0)
        mult_crossed(1, 0)
        mult_plain(1, 1)
        mult_crossed(1, 1)
        quantise(0, GROUP, GROUP)
        mx_straight(0, 2)
        mx_copy(0)
        prep_tables(1)
        mult_gpsimd(0)
        mult_plain(0, 2)
        mult_crossed(0, 2)
        add_straight(0, HEADS)
        mx_turned(0, 0)
        mx_turned(0, 1)
        next_v(2)
        mx_copy(1)
        mx_turned(0, 2)
        mult_gpsimd(1)
        mult_turned(0, 0)
        mx_turned(0, 3)
        mult_turned(0, 1)
        mx_turned(1, 0)
        next_v(2)
        back(0, 0)
        back(0, 1)
        store_first(0)
        prep_x(1, 0, 2)
        prep_x(1, 2, 2)
        mult_turned(0, 2)
        mx_turned(1, 1)
        mult_turned(0, 3)
        mx_turned(1, 2)
        next_v(2)
        mult_turned(1, 0)
        mx_straight(1, 2)
        swap_sin(2)
        prep_x(1, 4, 2)
        prep_x(1, 6, 2)
        back(0, 2)
        back(0, 3)
        store_rest(0)
        swap_sin(3)
        mult_turned(1, 1)
        mx_turned(1, 3)
        next_v(2)
        mult_turned(1, 2)
        mult_plain(1, 2)
        mult_crossed(1, 2, 1, HEADS)
        quantise(1, 0, PAIR)
        mult_crossed(1, 2, 0, 1)
        add_straight(1, HEADS)
        mx_straight(2, 0)
        mx_copy(2)
        mult_turned(1, 3)
        back(1, 0)
        back(1, 1)
        store_first(1)
        prep_tables(3)
        mx_straight(2, 1)
        mx_straight(2, 2)
        mx_turned(2, 0)
        next_v(2)

        final = ROUNDS - 1
        for r in range(2, final):
            even = r % 2 == 0
            pair = r // 2
            more = pair + 1 < N_PAIRS
            gate = more and not even
            next_is_final = r + 1 == final
            new_result(r)
            mult_gpsimd(r)
            mult_plain(r, 0)
            mult_crossed(r, 0)
            mult_plain(r, 1)
            mult_crossed(r, 1)
            mult_plain(r, 2)
            back(r - 1, 2)
            back(r - 1, 3)
            if more and even:
                prep_x(pair + 1, 0, 2)
                prep_x(pair + 1, 2, 2)
            store_rest(r - 1)
            if more:
                if even:
                    swap_sin(2 * pair + 2)
                else:
                    swap_sin(2 * pair + 3)
            if gate:
                mult_crossed(r, 2, 1, HEADS)
                quantise(pair + 1, 0, PAIR)
                mult_crossed(r, 2, 0, 1)
            else:
                mult_crossed(r, 2)
            add_straight(r, HEADS)
            mx_turned(r, 1)
            mx_turned(r, 2)
            next_v((0, 0, 2, 2, 2, 2, 2)[r])
            mx_copy(r + 1)
            mx_turned(r, 3)
            mult_turned(r, 0)
            if next_is_final:
                mx_turned(final, 0)
            else:
                mx_straight(r + 1, 0)
            mult_turned(r, 1)
            back(r, 0)
            back(r, 1)
            store_first(r)
            if more and even:
                prep_x(pair + 1, 4, 2)
                prep_x(pair + 1, 6, 2)
            if more and not even:
                prep_tables(2 * pair + 3)
            mult_turned(r, 2)
            mult_turned(r, 3)
            if next_is_final:
                mx_turned(final, 1)
                mx_turned(final, 2)
                mx_turned(final, 3)
            else:
                mx_straight(r + 1, 1)
                mx_straight(r + 1, 2)
                mx_turned(r + 1, 0)
            next_v((0, 0, 3, 2, 3, 3, 1)[r])

        new_result(final)
        mult_gpsimd(final)
        add_slot(nc.gpsimd, final, GROUP - 1)
        back(final - 1, 2)
        back(final - 1, 3)
        store_rest(final - 1)
        store_straight(final, (0, HEADS), (GROUP - 1, GROUP))
        for h in range(HEADS):
            mult_turned(final, h)
            if h < GROUP - 1:
                mx_straight(final, h)
            if h > 0:
                back(final, h - 1)
        back(final, HEADS - 1)
        for s in range(GROUP - 1):
            mult_plain(final, s)
            mult_crossed(final, s)
            if s < GROUP - 2:
                add_slot(nc.gpsimd, final, s)
        add_slot(nc.vector, final, GROUP - 2)
        store_turned(final, 0, 1)
        store_turned(final, 1, 1)
        store_straight(final, (0, HEADS), (0, 1))
        store_turned(final, 2, 1)
        store_turned(final, 3, 1)
        store_straight(final, (0, HEADS), (1, 2))
        store_straight(final, (0, HEADS), (2, 3))
